import numpy as np
import ml_dtypes


def mxq(x, axis, fmt="e4m3"):
    dtype, down = {"e4m3": (ml_dtypes.float8_e4m3fn, 7), "e5m2": (ml_dtypes.float8_e5m2, 14)}[fmt]
    v = np.moveaxis(np.asarray(x, np.float32).astype(ml_dtypes.bfloat16).astype(np.float64), axis, -1)
    blocks = v.reshape(v.shape[:-1] + (-1, 32))
    amax = np.abs(blocks).max(-1, keepdims=True)
    byte = np.maximum(np.where(amax > 0, np.frexp(amax)[1] - 1 + 127, 0) - down, 1)
    scale = np.exp2(byte - 127.0)
    codes = (blocks / scale).astype(np.float32).astype(dtype).astype(np.float64)
    return np.moveaxis((codes * scale).reshape(v.shape), -1, axis)


WIDE = False


def mx_kscale(k):
    if not WIDE:
        return np.ones(k)
    levels = np.array([10, -10, 5, -5, 0])
    if k % 512:
        return np.exp2(np.random.permutation(np.resize(levels, k // 32))).repeat(32)
    a = np.empty((k // 512, 16))
    for p in range(k // 512):
        a[p, :8] = np.random.permutation(np.resize(levels, 8))
        for g in range(8):
            far = levels[np.abs(levels - a[p, g]) >= 10]
            a[p, g + 8] = far[np.random.randint(len(far))]
    return np.exp2(a.ravel()).repeat(32)


BF16 = ml_dtypes.bfloat16


def bf(x):
    return np.asarray(x, np.float32).astype(BF16)


def f64(x):
    return np.asarray(x).astype(np.float64)


B, IN, H, OUT = 2048, 512, 512, 256
NG = 4
G = NG * H
X = IN - 1
Y = IN - X
EPS = 1e-5


def sigmoid(v):
    return 1.0 / (1.0 + np.exp(-v))


def bn(z, g, b):
    m = z.mean(axis=0)
    v = ((z - m) ** 2).mean(axis=0)
    return (z - m) / np.sqrt(v + EPS) * g + b


def setup_inputs():
    s, t = mx_kscale(IN), mx_kscale(H)
    return {
        "x": bf(np.random.standard_normal((B, X)) * s[:X]),
        "y": bf(np.random.standard_normal((B, Y)) * 3.0 * s[X:]),
        "h_prev": bf(np.random.standard_normal((B, H)) * t),
        "c_prev": bf(np.random.standard_normal((B, H))),
        "Wx": bf(np.random.standard_normal((G, IN)) / np.sqrt(IN) / s),
        "Wh": bf(np.random.standard_normal((G, H)) / np.sqrt(H) / t),
        "gx": bf(1.0 + 0.2 * np.random.standard_normal(G)),
        "bx": bf(0.2 * np.random.standard_normal(G)),
        "gh": bf(1.0 + 0.2 * np.random.standard_normal(G)),
        "bh": bf(0.2 * np.random.standard_normal(G)),
    }


def reference(x, y, h_prev, c_prev, Wx, Wh, gx, bx, gh, bh):
    inp = np.concatenate([f64(x), f64(y)], axis=1)
    zx = mxq(inp, 1, "e4m3") @ mxq(f64(Wx), 1, "e4m3").T
    zh = mxq(f64(h_prev), 1, "e4m3") @ mxq(f64(Wh), 1, "e4m3").T
    gates = bn(zx, f64(gx), f64(bx)) + bn(zh, f64(gh), f64(bh))
    f, i, o, g = np.split(gates, NG, axis=1)
    c_new = sigmoid(f) * f64(c_prev) + sigmoid(i) * np.tanh(g)
    h_new = sigmoid(o) * np.tanh(c_new)
    return h_new, c_new

@@ -1,0 +1,392 @@
+from contextlib import ExitStack
+
+import concourse.mybir as mybir
+from concourse.masks import make_identity
+
+F32 = mybir.dt.float32
+BF16 = mybir.dt.bfloat16
+U32 = mybir.dt.uint32
+U8 = mybir.dt.uint8
+FP8X4 = mybir.dt.float8_e4m3fn_x4
+ACT = mybir.ActivationFunctionType
+ALU = mybir.AluOpType
+
+P = 128
+PACK = 4
+BATCH = 2048
+FEATURES = P * PACK
+HIDDEN = 512
+GATES = 4
+F_GATE, I_GATE, O_GATE, G_GATE = 0, 1, 2, 3
+EPS = 1e-5
+
+ROW_TILES = BATCH // P
+CHUNK = 512
+CHUNKS = BATCH // CHUNK
+TILES_PER_CHUNK = CHUNK // P
+HIDDEN_TILES = HIDDEN // P
+GATE_TILES = GATES * HIDDEN_TILES
+WORDS = FEATURES // 2
+X_WHOLE_BLOCKS = 496
+STATS_DIM = 6
+
+FLOPS = 2 * 2 * BATCH * GATES * HIDDEN * FEATURES
+
+GATE_ORDER = (G_GATE, I_GATE, F_GATE, O_GATE)
+
+ITEMS = GATE_TILES * CHUNKS
+LEAD = 6
+HEAD_LAG = 2
+VECTOR_TILES = 2
+LAG_NORM_X = 2
+LAG_FUNCTION = 4
+LAG_FIRST_PRODUCT = 6
+LAG_SECOND_PRODUCT = 10
+LAG_TANH = 12
+LAG_STORE = 16
+SHORT_FIRST_PRODUCT = 5
+SHORT_SECOND_PRODUCT = 6
+SHORT_TANH = 7
+SHORT_STORE = 7
+
+
+def tile_cleanlstm_pa_kernel(tc, x, y, h_prev, c_prev, Wx, Wh, gx, bx, gh, bh, out_0, out_1):
+    nc = tc.nc
+    with ExitStack() as ctx:
+        ctx.enter_context(tc.manual_schedule())
+        const = ctx.enter_context(tc.tile_pool(name="const", bufs=1))
+        raw = ctx.enter_context(tc.tile_pool(name="raw", bufs=1))
+        keep = ctx.enter_context(tc.tile_pool(name="keep", bufs=1))
+        stage = ctx.enter_context(tc.tile_pool(name="stage", bufs=4))
+        small = ctx.enter_context(tc.tile_pool(name="small", bufs=5))
+        gates = ctx.enter_context(tc.tile_pool(name="gates", bufs=7))
+        rows_pool = ctx.enter_context(tc.tile_pool(name="rows", bufs=4))
+        psum = ctx.enter_context(tc.psum_pool(name="psum", bufs=8))
+
+        def chunk_cols(c):
+            return slice(c * CHUNK, (c + 1) * CHUNK)
+
+        def chunk_tiles(c):
+            return slice(c * TILES_PER_CHUNK, (c + 1) * TILES_PER_CHUNK)
+
+        x_sb = raw.tile([P, ROW_TILES * FEATURES], BF16)
+        x_rows = x_sb[:].rearrange("p (t k) -> p t k", t=ROW_TILES)
+        x_dram = x.rearrange("(p t) k -> p t k", t=ROW_TILES)
+        x_tail = raw.tile([P, ROW_TILES, 16], BF16)
+        y_sb = raw.tile([P, ROW_TILES], BF16)
+        h_sb = raw.tile([P, ROW_TILES * FEATURES], BF16)
+        h_rows = h_sb[:].rearrange("p (t k) -> p t k", t=ROW_TILES)
+        h_dram = h_prev.rearrange("(p t) k -> p t k", t=ROW_TILES)
+        c_sb = raw.tile([P, ROW_TILES, HIDDEN], BF16)
+        wx_sb = raw.tile([P, HIDDEN_TILES * GATES * FEATURES], BF16)
+        wh_sb = raw.tile([P, HIDDEN_TILES * GATES * FEATURES], BF16)
+        wx_rows = wx_sb[:].rearrange("p (j g k) -> p j g k", j=HIDDEN_TILES, g=GATES)
+        wh_rows = wh_sb[:].rearrange("p (j g k) -> p j g k", j=HIDDEN_TILES, g=GATES)
+        wx_dram = Wx.rearrange("(g j p) k -> p j g k", g=GATES, j=HIDDEN_TILES)
+        wh_dram = Wh.rearrange("(g j p) k -> p j g k", g=GATES, j=HIDDEN_TILES)
+
+        n_tail = FEATURES - 1 - X_WHOLE_BLOCKS
+        nc.scalar.dma_start(out=x_tail[:, :, 0:n_tail], in_=x_dram[:, :, X_WHOLE_BLOCKS : FEATURES - 1])
+        nc.scalar.dma_start(out=y_sb[:], in_=y.rearrange("(p t) o -> p (t o)", t=ROW_TILES))
+        par_rows = const.tile([P, P], BF16)
+        nc.vector.memset(par_rows[:], 0.0)
+        for q, vec in enumerate((gx, gh, bx, bh)):
+            nc.scalar.dma_start(
+                out=par_rows[q * GATE_TILES : (q + 1) * GATE_TILES, :], in_=vec.rearrange("(t p) -> t p", p=P)
+            )
+
+        nc.sync.dma_start(out=wx_rows[:, 0], in_=wx_dram[:, 0])
+        nc.sync.dma_start(out=wh_rows[:, 0], in_=wh_dram[:, 0])
+        for c in range(CHUNKS):
+            nc.sync.dma_start(
+                out=x_rows[:, chunk_tiles(c), 0:X_WHOLE_BLOCKS], in_=x_dram[:, chunk_tiles(c), 0:X_WHOLE_BLOCKS]
+            )
+        for c in range(CHUNKS):
+            nc.sync.dma_start(out=h_rows[:, chunk_tiles(c), :], in_=h_dram[:, chunk_tiles(c), :])
+        nc.sync.dma_start(out=wx_rows[:, 1], in_=wx_dram[:, 1])
+        nc.sync.dma_start(out=wh_rows[:, 1], in_=wh_dram[:, 1])
+        nc.sync.dma_start(out=c_sb[:], in_=c_prev.rearrange("(p t) k -> p t k", t=ROW_TILES))
+        for j in range(2, HIDDEN_TILES):
+            nc.sync.dma_start(out=wx_rows[:, j], in_=wx_dram[:, j])
+            nc.sync.dma_start(out=wh_rows[:, j], in_=wh_dram[:, j])
+
+        ident_f32 = const.tile([P, P], F32)
+        make_identity(nc, ident_f32[:])
+        ident_bf16 = const.tile([P, P], BF16)
+        make_identity(nc, ident_bf16[:])
+        minus_half = const.tile([P, 2], F32)
+        nc.gpsimd.memset(minus_half[:], -0.5)
+
+        nc.vector.tensor_copy(out=x_rows[:, :, X_WHOLE_BLOCKS : FEATURES - 1], in_=x_tail[:, :, 0:n_tail])
+        nc.vector.tensor_copy(out=x_rows[:, :, FEATURES - 1 : FEATURES], in_=y_sb[:].unsqueeze(2))
+
+        x_codes = keep.tile([P, BATCH], U32, align_bytes=64)
+        x_scales = keep.tile([P, BATCH], U8, align_bytes=64)
+        h_codes = keep.tile([P, BATCH], U32, align_bytes=64)
+        h_scales = keep.tile([P, BATCH], U8, align_bytes=64)
+        wx_codes = keep.tile([P, GATES * HIDDEN], U32, align_bytes=64)
+        wx_scales = keep.tile([P, GATES * HIDDEN], U8, align_bytes=64)
+        wh_codes = keep.tile([P, GATES * HIDDEN], U32, align_bytes=64)
+        wh_scales = keep.tile([P, GATES * HIDDEN], U8, align_bytes=64)
+
+        x_words = x_sb[:].bitcast(F32).rearrange("p (t w) -> p t w", w=WORDS)
+        h_words = h_sb[:].bitcast(F32).rearrange("p (t w) -> p t w", w=WORDS)
+        wx_words = wx_sb[:].bitcast(F32).rearrange("p (t w) -> p t w", w=WORDS)
+        wh_words = wh_sb[:].bitcast(F32).rearrange("p (t w) -> p t w", w=WORDS)
+
+        def new_grouped():
+            grouped = stage.tile([P, CHUNK * PACK], BF16, tag="grouped", align_bytes=64)
+            return grouped
+
+        def transpose_256_rows(words, c, a, grouped):
+            grouped_words = grouped[:].bitcast(F32).rearrange("p (a t r u) -> p a t r u", a=2, t=2, u=2)
+            bank = psum.tile([P, 2, 2, P], F32, tag="bank")
+            for t in range(2):
+                for u in range(2):
+                    nc.tensor.transpose(
+                        bank[:, t, u, :], words[:, c * TILES_PER_CHUNK + 2 * a + t, u : 2 * P : 2], ident_f32[:]
+                    )
+            nc.scalar.copy(out=grouped_words[:, a], in_=bank[:].rearrange("p t u r -> p t r u"))
+
+        def quantise(grouped, codes, scales, c):
+            nc.vector.quantize_mx(
+                out=codes[:, chunk_cols(c)].bitcast(FP8X4), scales=scales[:, chunk_cols(c)], in_=grouped[:]
+            )
+
+        def quantise_chunk(words, codes, scales, c):
+            grouped = new_grouped()
+            for a in range(2):
+                transpose_256_rows(words, c, a, grouped)
+            quantise(grouped, codes, scales, c)
+
+        operands = (
+            (wx_codes, wx_scales, x_codes, x_scales),
+            (wh_codes, wh_scales, h_codes, h_scales),
+        )
+        order = [(j, gate) for j in range(HIDDEN_TILES) for gate in GATE_ORDER]
+
+        def project(s, n, c):
+            j, gate = order[n]
+            w_codes, w_scales, a_codes, a_scales = operands[s]
+            w_cols = slice((j * GATES + gate) * P, (j * GATES + gate + 1) * P)
+            z = psum.tile([P, CHUNK], F32, tag="bank")
+            nc.tensor.matmul_mx(
+                out=z[:],
+                lhsT=w_codes[:, w_cols].bitcast(FP8X4),
+                lhsT_scale=w_scales[:, w_cols],
+                rhs=a_codes[:, chunk_cols(c)].bitcast(FP8X4),
+                rhs_scale=a_scales[:, chunk_cols(c)],
+                start=True,
+                stop=True,
+            )
+            return z
+
+        stats = {}
+        slopes = {}
+        shifts = {}
+        values = {}
+
+        def chunk_statistics(s, n, c):
+            z = project(s, n, c)
+            nc.vector.bn_stats(out=stats[n][:, s, c, :], in_=z[:])
+
+        def coefficients(n):
+            j, gate = order[n]
+            t = gate * HIDDEN_TILES + j
+            mean_var = small.tile([P, 2, 2], F32, tag="mean_var")
+            for s in range(2):
+                nc.vector.bn_aggr(out=mean_var[:, s, :], in_=stats[n][:, s, :, :].rearrange("p c k -> p (c k)"))
+            rstd = small.tile([P, 2], F32, tag="rstd")
+            nc.gpsimd.tensor_scalar(
+                out=rstd[:], in0=mean_var[:, :, 1], scalar1=1.0, scalar2=EPS, op0=ALU.mult, op1=ALU.add
+            )
+            nc.gpsimd.tensor_tensor(out=rstd[:], in0=rstd[:], in1=minus_half[:], op=ALU.pow)
+            slope = small.tile([P, 2], F32, tag="slope")
+            nc.gpsimd.tensor_tensor(out=slope[:], in0=rstd[:], in1=par[:, 0:2, t], op=ALU.mult)
+            shift = small.tile([P, 2], F32, tag="shift")
+            nc.gpsimd.tensor_tensor(out=shift[:], in0=mean_var[:, :, 0], in1=slope[:], op=ALU.mult)
+            nc.gpsimd.tensor_tensor(out=shift[:], in0=par[:, 2:4, t], in1=shift[:], op=ALU.subtract)
+            slopes[n] = slope
+            shifts[n] = shift
+
+        def new_stats(n):
+            stats_n = small.tile([P, 2, CHUNKS, STATS_DIM], F32, tag="stats")
+            stats[n] = stats_n
+
+        quantise_chunk(wx_words, wx_codes, wx_scales, 0)
+        quantise_chunk(wh_words, wh_codes, wh_scales, 0)
+        par_bank = psum.tile([P, P], BF16, tag="bank")
+        nc.tensor.transpose(par_bank[:], par_rows[:], ident_bf16[:])
+        par = const.tile([P, 4, GATE_TILES], F32)
+        nc.vector.tensor_copy(out=par[:].rearrange("p q t -> p (q t)"), in_=par_bank[:, 0 : 4 * GATE_TILES])
+        head_items = [divmod(i, CHUNKS) for i in range(LEAD)]
+        for n, c in head_items:
+            if c == 0:
+                new_stats(n)
+        activations = ((x_words, x_codes, x_scales), (h_words, h_codes, h_scales))
+        head_chunks = [(s, chunk) for s in range(2) for chunk in range(CHUNKS)]
+        for k in range(len(head_chunks) + HEAD_LAG):
+            if k < len(head_chunks):
+                s, chunk = head_chunks[k]
+                quantise_chunk(*activations[s], chunk)
+            if k >= HEAD_LAG:
+                s, chunk = head_chunks[k - HEAD_LAG]
+                for n, c in head_items:
+                    if c == chunk:
+                        chunk_statistics(s, n, c)
+        for n, c in head_items:
+            if c == CHUNKS - 1:
+                coefficients(n)
+
+        cell_t = keep.tile([P, HIDDEN_TILES, BATCH], BF16)
+        half_tiles = ROW_TILES // 2
+        next_grouped = {}
+
+        def first_sweep(i):
+            if i >= ITEMS:
+                return
+            n, c = divmod(i, CHUNKS)
+            if c == 0:
+                new_stats(n)
+            for s in range(2):
+                chunk_statistics(s, n, c)
+            if c == CHUNKS - 1:
+                coefficients(n)
+
+        def norm_h(i):
+            if i >= ITEMS:
+                return
+            n, c = divmod(i, CHUNKS)
+            if c == 0:
+                value = gates.tile([P, BATCH], F32, tag="gate")
+                values[n] = value
+            zh = project(1, n, c)
+            nc.scalar.activation(
+                out=values[n][:, chunk_cols(c)],
+                in_=zh[:],
+                func=ACT.Identity,
+                scale=slopes[n][:, 1:2],
+                bias=shifts[n][:, 1:2],
+            )
+
+        def norm_x(i):
+            if i < 0 or i >= ITEMS:
+                return
+            n, c = divmod(i, CHUNKS)
+            part = values[n][:, chunk_cols(c)]
+            zx = project(0, n, c)
+            nc.vector.scalar_tensor_tensor(
+                out=part, in0=zx[:], scalar=slopes[n][:, 0:1], in1=part, op0=ALU.mult, op1=ALU.add
+            )
+
+        def gate_function(i):
+            if i < 0 or i >= ITEMS:
+                return
+            n, c = divmod(i, CHUNKS)
+            part = values[n][:, chunk_cols(c)]
+            func = ACT.Tanh if order[n][1] == G_GATE else ACT.Sigmoid
+            nc.scalar.activation(out=part, in_=part, func=func, bias=shifts[n][:, 0:1])
+
+        def vector_is_free(n):
+            return n + VECTOR_TILES >= GATE_TILES
+
+        def due(i, lag, short_lag):
+            items = []
+            for item, on_vector in ((i - lag, False), (i - short_lag, True)):
+                if 0 <= item < ITEMS and vector_is_free(item // CHUNKS) == on_vector:
+                    items.append(item)
+            return items
+
+        def products_engine(n):
+            return nc.vector if vector_is_free(n) else nc.gpsimd
+
+        def first_product(i):
+            n, c = divmod(i, CHUNKS)
+            j, gate = order[n]
+            cols = chunk_cols(c)
+            mine = values[n][:, cols]
+            candidate = values[j * GATES][:, cols]
+            if gate == I_GATE:
+                products_engine(n).tensor_tensor(out=candidate, in0=mine, in1=candidate, op=ALU.mult)
+            if gate == F_GATE:
+                products_engine(n).tensor_tensor(out=mine, in0=mine, in1=cell_t[:, j, cols], op=ALU.mult)
+
+        def second_product(i):
+            n, c = divmod(i, CHUNKS)
+            j, gate = order[n]
+            cols = chunk_cols(c)
+            mine = values[n][:, cols]
+            candidate = values[j * GATES][:, cols]
+            if gate == F_GATE:
+                products_engine(n).tensor_tensor(out=mine, in0=mine, in1=candidate, op=ALU.add)
+            if gate == O_GATE:
+                products_engine(n).tensor_tensor(out=mine, in0=mine, in1=candidate, op=ALU.mult)
+
+        def cell_tanh(i):
+            n, c = divmod(i, CHUNKS)
+            j, gate = order[n]
+            if gate == F_GATE:
+                nc.scalar.activation(
+                    out=values[j * GATES][:, chunk_cols(c)], in_=values[n][:, chunk_cols(c)], func=ACT.Tanh
+                )
+
+        def store(i):
+            n, c = divmod(i, CHUNKS)
+            j, gate = order[n]
+            if gate != F_GATE and gate != O_GATE:
+                return
+            out = out_1 if gate == F_GATE else out_0
+            bank = psum.tile([P, TILES_PER_CHUNK, P], F32, tag="bank")
+            for t in range(TILES_PER_CHUNK):
+                first = (c * TILES_PER_CHUNK + t) * P
+                nc.tensor.transpose(bank[:, t, :], values[n][:, first : first + P], ident_f32[:])
+            rows = rows_pool.tile([P, TILES_PER_CHUNK, P], F32, tag="rows")
+            if vector_is_free(n):
+                nc.vector.tensor_copy(out=rows[:], in_=bank[:])
+            else:
+                nc.scalar.copy(out=rows[:], in_=bank[:])
+            out_rows = out.rearrange("(p t) k -> p t k", t=ROW_TILES)
+            nc.sync.dma_start(out=out_rows[:, chunk_tiles(c), j * P : (j + 1) * P], in_=rows[:])
+
+        def prepare(i):
+            if i >= ITEMS:
+                return
+            n, c = divmod(i, CHUNKS)
+            j, gate = order[n]
+            if gate == G_GATE and j + 1 < HIDDEN_TILES:
+                s, a = divmod(c, 2)
+                if a == 0:
+                    next_grouped[s] = new_grouped()
+                transpose_256_rows((wx_words, wh_words)[s], j + 1, a, next_grouped[s])
+            if gate == I_GATE and c == 0 and j + 1 < HIDDEN_TILES:
+                quantise(next_grouped[0], wx_codes, wx_scales, j + 1)
+                quantise(next_grouped[1], wh_codes, wh_scales, j + 1)
+            if j == 0 and (gate == I_GATE or gate == F_GATE):
+                jc, a = divmod(i - CHUNKS, 2)
+                bank = psum.tile([P, half_tiles, P], BF16, tag="bank")
+                for t in range(half_tiles):
+                    nc.tensor.transpose(bank[:, t, :], c_sb[:, a * half_tiles + t, jc * P : (jc + 1) * P], ident_bf16[:])
+                nc.scalar.copy(
+                    out=cell_t[:, jc, a * half_tiles * P : (a + 1) * half_tiles * P],
+                    in_=bank[:].rearrange("p t r -> p (t r)"),
+                )
+
+        for i in range(ITEMS + LAG_STORE):
+            if i % 2 == 1:
+                for item in due(i, LAG_STORE, SHORT_STORE):
+                    store(item)
+                prepare(i)
+            norm_x(i - LAG_NORM_X)
+            first_sweep(i + LEAD)
+            norm_h(i)
+            gate_function(i - LAG_FUNCTION)
+            for item in due(i, LAG_FIRST_PRODUCT, SHORT_FIRST_PRODUCT):
+                first_product(item)
+            for item in due(i, LAG_SECOND_PRODUCT, SHORT_SECOND_PRODUCT):
+                second_product(item)
+            for item in due(i, LAG_TANH, SHORT_TANH):
+                cell_tanh(item)
+            if i % 2 == 0:
+                for item in due(i, LAG_STORE, SHORT_STORE):
+                    store(item)
+                prepare(i)

@@ -35,19 +35,19 @@ FLOPS = 2 * 2 * BATCH * GATES * HIDDEN * FEATURES
 GATE_ORDER = (G_GATE, I_GATE, F_GATE, O_GATE)
 
 ITEMS = GATE_TILES * CHUNKS
+PAIR = 2
 LEAD = 6
 HEAD_LAG = 2
 VECTOR_TILES = 2
 LAG_NORM_X = 2
-LAG_FUNCTION = 4
-LAG_FIRST_PRODUCT = 6
-LAG_SECOND_PRODUCT = 10
-LAG_TANH = 12
-LAG_STORE = 16
-SHORT_FIRST_PRODUCT = 5
-SHORT_SECOND_PRODUCT = 6
-SHORT_TANH = 7
-SHORT_STORE = 7
+LAG_TURN = 6
+LAG_FIRST_PRODUCT = LAG_TURN + 2
+LAG_SECOND_PRODUCT = LAG_TURN + 6
+LAG_TANH = LAG_TURN + 8
+SHORT_PRODUCT = LAG_TURN
+SHORT_TANH = LAG_TURN + 2
+LAST_LAG = LAG_TANH
+SPLIT = (1, 3)
 
 
 def tile_cleanlstm_pa_kernel(tc, x, y, h_prev, c_prev, Wx, Wh, gx, bx, gh, bh, out_0, out_1):
@@ -60,7 +60,7 @@ def tile_cleanlstm_pa_kernel(tc, x, y, h_prev, c_prev, Wx, Wh, gx, bx, gh, bh, o
         stage = ctx.enter_context(tc.tile_pool(name="stage", bufs=4))
         small = ctx.enter_context(tc.tile_pool(name="small", bufs=5))
         gates = ctx.enter_context(tc.tile_pool(name="gates", bufs=7))
-        rows_pool = ctx.enter_context(tc.tile_pool(name="rows", bufs=4))
+        sums = ctx.enter_context(tc.tile_pool(name="sums", bufs=14))
         psum = ctx.enter_context(tc.psum_pool(name="psum", bufs=8))
 
         def chunk_cols(c):
@@ -184,6 +184,8 @@ def tile_cleanlstm_pa_kernel(tc, x, y, h_prev, c_prev, Wx, Wh, gx, bx, gh, bh, o
         stats = {}
         slopes = {}
         shifts = {}
+        norms = {}
+        others = {}
         values = {}
 
         def chunk_statistics(s, n, c):
@@ -203,9 +205,10 @@ def tile_cleanlstm_pa_kernel(tc, x, y, h_prev, c_prev, Wx, Wh, gx, bx, gh, bh, o
             nc.gpsimd.tensor_tensor(out=rstd[:], in0=rstd[:], in1=minus_half[:], op=ALU.pow)
             slope = small.tile([P, 2], F32, tag="slope")
             nc.gpsimd.tensor_tensor(out=slope[:], in0=rstd[:], in1=par[:, 0:2, t], op=ALU.mult)
-            shift = small.tile([P, 2], F32, tag="shift")
-            nc.gpsimd.tensor_tensor(out=shift[:], in0=mean_var[:, :, 0], in1=slope[:], op=ALU.mult)
-            nc.gpsimd.tensor_tensor(out=shift[:], in0=par[:, 2:4, t], in1=shift[:], op=ALU.subtract)
+            shift = small.tile([P, 3], F32, tag="shift")
+            nc.gpsimd.tensor_tensor(out=shift[:, 0:2], in0=mean_var[:, :, 0], in1=slope[:], op=ALU.mult)
+            nc.gpsimd.tensor_tensor(out=shift[:, 0:2], in0=par[:, 2:4, t], in1=shift[:, 0:2], op=ALU.subtract)
+            nc.gpsimd.tensor_tensor(out=shift[:, 2:3], in0=shift[:, 0:1], in1=shift[:, 1:2], op=ALU.add)
             slopes[n] = slope
             shifts[n] = shift
 
@@ -238,13 +241,9 @@ def tile_cleanlstm_pa_kernel(tc, x, y, h_prev, c_prev, Wx, Wh, gx, bx, gh, bh, o
             if c == CHUNKS - 1:
                 coefficients(n)
 
-        cell_t = keep.tile([P, HIDDEN_TILES, BATCH], BF16)
-        half_tiles = ROW_TILES // 2
         next_grouped = {}
 
         def first_sweep(i):
-            if i >= ITEMS:
-                return
             n, c = divmod(i, CHUNKS)
             if c == 0:
                 new_stats(n)
@@ -254,48 +253,54 @@ def tile_cleanlstm_pa_kernel(tc, x, y, h_prev, c_prev, Wx, Wh, gx, bx, gh, bh, o
                 coefficients(n)
 
         def norm_h(i):
-            if i >= ITEMS:
-                return
             n, c = divmod(i, CHUNKS)
-            if c == 0:
-                value = gates.tile([P, BATCH], F32, tag="gate")
-                values[n] = value
+            norm = sums.tile([P, CHUNK], F32, tag="norm")
+            norms[i] = norm
             zh = project(1, n, c)
             nc.scalar.activation(
-                out=values[n][:, chunk_cols(c)],
-                in_=zh[:],
-                func=ACT.Identity,
-                scale=slopes[n][:, 1:2],
-                bias=shifts[n][:, 1:2],
+                out=norm[:], in_=zh[:], func=ACT.Identity, scale=slopes[n][:, 1:2], bias=shifts[n][:, 2:3]
             )
 
         def norm_x(i):
-            if i < 0 or i >= ITEMS:
-                return
             n, c = divmod(i, CHUNKS)
-            part = values[n][:, chunk_cols(c)]
             zx = project(0, n, c)
+            if c in SPLIT:
+                other = sums.tile([P, CHUNK], F32, tag="norm_x", bufs=6)
+                nc.scalar.activation(out=other[:], in_=zx[:], func=ACT.Identity, scale=slopes[n][:, 0:1])
+                others[i] = other
+                return
             nc.vector.scalar_tensor_tensor(
-                out=part, in0=zx[:], scalar=slopes[n][:, 0:1], in1=part, op0=ALU.mult, op1=ALU.add
+                out=norms[i][:], in0=zx[:], scalar=slopes[n][:, 0:1], in1=norms[i][:], op0=ALU.mult, op1=ALU.add
             )
 
-        def gate_function(i):
-            if i < 0 or i >= ITEMS:
-                return
+        def turn(i):
+            bank = psum.tile([P, TILES_PER_CHUNK, P], F32, tag="bank")
+            for t in range(TILES_PER_CHUNK):
+                cols = slice(t * P, (t + 1) * P)
+                if i in others:
+                    nc.tensor.matmul(bank[:, t, :], lhsT=norms[i][:, cols], rhs=ident_f32[:], is_transpose=True, start=True, stop=False)
+                    nc.tensor.matmul(bank[:, t, :], lhsT=others[i][:, cols], rhs=ident_f32[:], is_transpose=True, start=False, stop=True)
+                else:
+                    nc.tensor.transpose(bank[:, t, :], norms[i][:, cols], ident_f32[:])
+            return bank
+
+        def gate_function(i, bank):
             n, c = divmod(i, CHUNKS)
-            part = values[n][:, chunk_cols(c)]
+            if c == 0:
+                value = gates.tile([P, ROW_TILES, P], F32, tag="gate")
+                values[n] = value
             func = ACT.Tanh if order[n][1] == G_GATE else ACT.Sigmoid
-            nc.scalar.activation(out=part, in_=part, func=func, bias=shifts[n][:, 0:1])
+            nc.scalar.activation(out=values[n][:, chunk_tiles(c), :], in_=bank[:], func=func)
 
         def vector_is_free(n):
             return n + VECTOR_TILES >= GATE_TILES
 
+        def pair(i, lag):
+            return [item for item in range(i - lag, i - lag + PAIR) if 0 <= item < ITEMS]
+
         def due(i, lag, short_lag):
-            items = []
-            for item, on_vector in ((i - lag, False), (i - short_lag, True)):
-                if 0 <= item < ITEMS and vector_is_free(item // CHUNKS) == on_vector:
-                    items.append(item)
-            return items
+            late = [item for item in pair(i, lag) if not vector_is_free(item // CHUNKS)]
+            return late + [item for item in pair(i, short_lag) if vector_is_free(item // CHUNKS)]
 
         def products_engine(n):
             return nc.vector if vector_is_free(n) else nc.gpsimd
@@ -303,90 +308,64 @@ def tile_cleanlstm_pa_kernel(tc, x, y, h_prev, c_prev, Wx, Wh, gx, bx, gh, bh, o
         def first_product(i):
             n, c = divmod(i, CHUNKS)
             j, gate = order[n]
-            cols = chunk_cols(c)
-            mine = values[n][:, cols]
-            candidate = values[j * GATES][:, cols]
+            mine = values[n][:, chunk_tiles(c), :]
             if gate == I_GATE:
+                candidate = values[j * GATES][:, chunk_tiles(c), :]
                 products_engine(n).tensor_tensor(out=candidate, in0=mine, in1=candidate, op=ALU.mult)
             if gate == F_GATE:
-                products_engine(n).tensor_tensor(out=mine, in0=mine, in1=cell_t[:, j, cols], op=ALU.mult)
+                cell = c_sb[:, chunk_tiles(c), j * P : (j + 1) * P]
+                products_engine(n).tensor_tensor(out=mine, in0=mine, in1=cell, op=ALU.mult)
 
         def second_product(i):
             n, c = divmod(i, CHUNKS)
             j, gate = order[n]
-            cols = chunk_cols(c)
-            mine = values[n][:, cols]
-            candidate = values[j * GATES][:, cols]
-            if gate == F_GATE:
-                products_engine(n).tensor_tensor(out=mine, in0=mine, in1=candidate, op=ALU.add)
-            if gate == O_GATE:
-                products_engine(n).tensor_tensor(out=mine, in0=mine, in1=candidate, op=ALU.mult)
+            if gate != F_GATE and gate != O_GATE:
+                return
+            mine = values[n][:, chunk_tiles(c), :]
+            candidate = values[j * GATES][:, chunk_tiles(c), :]
+            op, out = (ALU.add, out_1) if gate == F_GATE else (ALU.mult, out_0)
+            products_engine(n).tensor_tensor(out=mine, in0=mine, in1=candidate, op=op)
+            out_rows = out.rearrange("(p t) k -> p t k", t=ROW_TILES)
+            nc.sync.dma_start(out=out_rows[:, chunk_tiles(c), j * P : (j + 1) * P], in_=mine)
 
         def cell_tanh(i):
             n, c = divmod(i, CHUNKS)
             j, gate = order[n]
             if gate == F_GATE:
                 nc.scalar.activation(
-                    out=values[j * GATES][:, chunk_cols(c)], in_=values[n][:, chunk_cols(c)], func=ACT.Tanh
+                    out=values[j * GATES][:, chunk_tiles(c), :], in_=values[n][:, chunk_tiles(c), :], func=ACT.Tanh
                 )
 
-        def store(i):
-            n, c = divmod(i, CHUNKS)
-            j, gate = order[n]
-            if gate != F_GATE and gate != O_GATE:
-                return
-            out = out_1 if gate == F_GATE else out_0
-            bank = psum.tile([P, TILES_PER_CHUNK, P], F32, tag="bank")
-            for t in range(TILES_PER_CHUNK):
-                first = (c * TILES_PER_CHUNK + t) * P
-                nc.tensor.transpose(bank[:, t, :], values[n][:, first : first + P], ident_f32[:])
-            rows = rows_pool.tile([P, TILES_PER_CHUNK, P], F32, tag="rows")
-            if vector_is_free(n):
-                nc.vector.tensor_copy(out=rows[:], in_=bank[:])
-            else:
-                nc.scalar.copy(out=rows[:], in_=bank[:])
-            out_rows = out.rearrange("(p t) k -> p t k", t=ROW_TILES)
-            nc.sync.dma_start(out=out_rows[:, chunk_tiles(c), j * P : (j + 1) * P], in_=rows[:])
-
         def prepare(i):
-            if i >= ITEMS:
-                return
             n, c = divmod(i, CHUNKS)
             j, gate = order[n]
-            if gate == G_GATE and j + 1 < HIDDEN_TILES:
+            if j + 1 == HIDDEN_TILES:
+                return
+            if gate == G_GATE:
                 s, a = divmod(c, 2)
                 if a == 0:
                     next_grouped[s] = new_grouped()
                 transpose_256_rows((wx_words, wh_words)[s], j + 1, a, next_grouped[s])
-            if gate == I_GATE and c == 0 and j + 1 < HIDDEN_TILES:
+            if gate == I_GATE and c == 0:
                 quantise(next_grouped[0], wx_codes, wx_scales, j + 1)
                 quantise(next_grouped[1], wh_codes, wh_scales, j + 1)
-            if j == 0 and (gate == I_GATE or gate == F_GATE):
-                jc, a = divmod(i - CHUNKS, 2)
-                bank = psum.tile([P, half_tiles, P], BF16, tag="bank")
-                for t in range(half_tiles):
-                    nc.tensor.transpose(bank[:, t, :], c_sb[:, a * half_tiles + t, jc * P : (jc + 1) * P], ident_bf16[:])
-                nc.scalar.copy(
-                    out=cell_t[:, jc, a * half_tiles * P : (a + 1) * half_tiles * P],
-                    in_=bank[:].rearrange("p t r -> p (t r)"),
-                )
 
-        for i in range(ITEMS + LAG_STORE):
-            if i % 2 == 1:
-                for item in due(i, LAG_STORE, SHORT_STORE):
-                    store(item)
-                prepare(i)
-            norm_x(i - LAG_NORM_X)
-            first_sweep(i + LEAD)
-            norm_h(i)
-            gate_function(i - LAG_FUNCTION)
-            for item in due(i, LAG_FIRST_PRODUCT, SHORT_FIRST_PRODUCT):
+        for i in range(0, ITEMS + LAST_LAG, PAIR):
+            turned = [(item, turn(item)) for item in pair(i, LAG_TURN)]
+            for item, bank in turned:
+                gate_function(item, bank)
+            for item in pair(i, 0):
+                prepare(item)
+            for k in range(PAIR):
+                if i + k - LAG_NORM_X in range(ITEMS):
+                    norm_x(i + k - LAG_NORM_X)
+                if i + k + LEAD < ITEMS:
+                    first_sweep(i + k + LEAD)
+                if i + k < ITEMS:
+                    norm_h(i + k)
+            for item in due(i, LAG_FIRST_PRODUCT, SHORT_PRODUCT):
                 first_product(item)
-            for item in due(i, LAG_SECOND_PRODUCT, SHORT_SECOND_PRODUCT):
+            for item in due(i, LAG_SECOND_PRODUCT, SHORT_PRODUCT):
                 second_product(item)
             for item in due(i, LAG_TANH, SHORT_TANH):
                 cell_tanh(item)
-            if i % 2 == 0:
-                for item in due(i, LAG_STORE, SHORT_STORE):
-                    store(item)
-                prepare(i)

@@ -32,22 +32,24 @@ STATS_DIM = 6
 
 FLOPS = 2 * 2 * BATCH * GATES * HIDDEN * FEATURES
 
-GATE_ORDER = (G_GATE, I_GATE, F_GATE, O_GATE)
+GATE_ORDER = (I_GATE, G_GATE, F_GATE, O_GATE)
 
 ITEMS = GATE_TILES * CHUNKS
 PAIR = 2
-LEAD = 6
+LEAD = 10
 HEAD_LAG = 2
+SPLIT_CHUNKS = (1, 3)
 VECTOR_TILES = 2
 LAG_NORM_X = 2
-LAG_TURN = 6
-LAG_FIRST_PRODUCT = LAG_TURN + 2
-LAG_SECOND_PRODUCT = LAG_TURN + 6
+LAG_TURN = 4
+LAG_CANDIDATE = LAG_TURN
+LAG_CELL = LAG_TURN + 4
 LAG_TANH = LAG_TURN + 8
+LAG_HIDDEN = LAG_TURN + 6
 SHORT_PRODUCT = LAG_TURN
 SHORT_TANH = LAG_TURN + 2
 LAST_LAG = LAG_TANH
-SPLIT = (1, 3)
+VALUE_TILES = {I_GATE: 8, G_GATE: 4, F_GATE: 6, O_GATE: 6}
 
 
 def tile_cleanlstm_pa_kernel(tc, x, y, h_prev, c_prev, Wx, Wh, gx, bx, gh, bh, out_0, out_1):
@@ -58,9 +60,9 @@ def tile_cleanlstm_pa_kernel(tc, x, y, h_prev, c_prev, Wx, Wh, gx, bx, gh, bh, o
         raw = ctx.enter_context(tc.tile_pool(name="raw", bufs=1))
         keep = ctx.enter_context(tc.tile_pool(name="keep", bufs=1))
         stage = ctx.enter_context(tc.tile_pool(name="stage", bufs=4))
-        small = ctx.enter_context(tc.tile_pool(name="small", bufs=5))
-        gates = ctx.enter_context(tc.tile_pool(name="gates", bufs=7))
-        sums = ctx.enter_context(tc.tile_pool(name="sums", bufs=14))
+        small = ctx.enter_context(tc.tile_pool(name="small", bufs=4))
+        sums = ctx.enter_context(tc.tile_pool(name="sums", bufs=8))
+        gates = ctx.enter_context(tc.tile_pool(name="gates", bufs=8))
         psum = ctx.enter_context(tc.psum_pool(name="psum", bufs=8))
 
         def chunk_cols(c):
@@ -95,14 +97,17 @@ def tile_cleanlstm_pa_kernel(tc, x, y, h_prev, c_prev, Wx, Wh, gx, bx, gh, bh, o
                 out=par_rows[q * GATE_TILES : (q + 1) * GATE_TILES, :], in_=vec.rearrange("(t p) -> t p", p=P)
             )
 
-        nc.sync.dma_start(out=wx_rows[:, 0], in_=wx_dram[:, 0])
-        nc.sync.dma_start(out=wh_rows[:, 0], in_=wh_dram[:, 0])
+        nc.sync.dma_start(out=wx_rows[:, 0, GATE_ORDER[0]], in_=wx_dram[:, 0, GATE_ORDER[0]])
+        nc.sync.dma_start(out=wh_rows[:, 0, GATE_ORDER[0]], in_=wh_dram[:, 0, GATE_ORDER[0]])
         for c in range(CHUNKS):
             nc.sync.dma_start(
                 out=x_rows[:, chunk_tiles(c), 0:X_WHOLE_BLOCKS], in_=x_dram[:, chunk_tiles(c), 0:X_WHOLE_BLOCKS]
             )
         for c in range(CHUNKS):
             nc.sync.dma_start(out=h_rows[:, chunk_tiles(c), :], in_=h_dram[:, chunk_tiles(c), :])
+        for gate in GATE_ORDER[1:]:
+            nc.sync.dma_start(out=wx_rows[:, 0, gate], in_=wx_dram[:, 0, gate])
+            nc.sync.dma_start(out=wh_rows[:, 0, gate], in_=wh_dram[:, 0, gate])
         nc.sync.dma_start(out=wx_rows[:, 1], in_=wx_dram[:, 1])
         nc.sync.dma_start(out=wh_rows[:, 1], in_=wh_dram[:, 1])
         nc.sync.dma_start(out=c_sb[:], in_=c_prev.rearrange("(p t) k -> p t k", t=ROW_TILES))
@@ -114,7 +119,7 @@ def tile_cleanlstm_pa_kernel(tc, x, y, h_prev, c_prev, Wx, Wh, gx, bx, gh, bh, o
         make_identity(nc, ident_f32[:])
         ident_bf16 = const.tile([P, P], BF16)
         make_identity(nc, ident_bf16[:])
-        minus_half = const.tile([P, 2], F32)
+        minus_half = const.tile([P, 2, 2], F32)
         nc.gpsimd.memset(minus_half[:], -0.5)
 
         nc.vector.tensor_copy(out=x_rows[:, :, X_WHOLE_BLOCKS : FEATURES - 1], in_=x_tail[:, :, 0:n_tail])
@@ -124,248 +129,246 @@ def tile_cleanlstm_pa_kernel(tc, x, y, h_prev, c_prev, Wx, Wh, gx, bx, gh, bh, o
         x_scales = keep.tile([P, BATCH], U8, align_bytes=64)
         h_codes = keep.tile([P, BATCH], U32, align_bytes=64)
         h_scales = keep.tile([P, BATCH], U8, align_bytes=64)
-        wx_codes = keep.tile([P, GATES * HIDDEN], U32, align_bytes=64)
-        wx_scales = keep.tile([P, GATES * HIDDEN], U8, align_bytes=64)
-        wh_codes = keep.tile([P, GATES * HIDDEN], U32, align_bytes=64)
-        wh_scales = keep.tile([P, GATES * HIDDEN], U8, align_bytes=64)
+        w_codes = keep.tile([P, GATE_TILES * 2 * P], U32, align_bytes=64)
+        w_scales = keep.tile([P, GATE_TILES * 2 * P], U8, align_bytes=64)
 
         x_words = x_sb[:].bitcast(F32).rearrange("p (t w) -> p t w", w=WORDS)
         h_words = h_sb[:].bitcast(F32).rearrange("p (t w) -> p t w", w=WORDS)
         wx_words = wx_sb[:].bitcast(F32).rearrange("p (t w) -> p t w", w=WORDS)
         wh_words = wh_sb[:].bitcast(F32).rearrange("p (t w) -> p t w", w=WORDS)
+        activations = ((x_words, x_codes, x_scales), (h_words, h_codes, h_scales))
+        order = [(j, gate) for j in range(HIDDEN_TILES) for gate in GATE_ORDER]
 
         def new_grouped():
             grouped = stage.tile([P, CHUNK * PACK], BF16, tag="grouped", align_bytes=64)
             return grouped
 
-        def transpose_256_rows(words, c, a, grouped):
+        def transpose_256_rows(blocks, grouped, a):
             grouped_words = grouped[:].bitcast(F32).rearrange("p (a t r u) -> p a t r u", a=2, t=2, u=2)
             bank = psum.tile([P, 2, 2, P], F32, tag="bank")
-            for t in range(2):
+            for t, words in enumerate(blocks):
                 for u in range(2):
-                    nc.tensor.transpose(
-                        bank[:, t, u, :], words[:, c * TILES_PER_CHUNK + 2 * a + t, u : 2 * P : 2], ident_f32[:]
-                    )
+                    nc.tensor.transpose(bank[:, t, u, :], words[:, u : 2 * P : 2], ident_f32[:])
             nc.scalar.copy(out=grouped_words[:, a], in_=bank[:].rearrange("p t u r -> p t r u"))
 
-        def quantise(grouped, codes, scales, c):
+        def prepare_chunk(s, c):
+            words, codes, scales = activations[s]
+            grouped = new_grouped()
+            for a in range(2):
+                first = c * TILES_PER_CHUNK + 2 * a
+                transpose_256_rows((words[:, first], words[:, first + 1]), grouped, a)
             nc.vector.quantize_mx(
                 out=codes[:, chunk_cols(c)].bitcast(FP8X4), scales=scales[:, chunk_cols(c)], in_=grouped[:]
             )
 
-        def quantise_chunk(words, codes, scales, c):
-            grouped = new_grouped()
-            for a in range(2):
-                transpose_256_rows(words, c, a, grouped)
-            quantise(grouped, codes, scales, c)
+        def transpose_weights(n, grouped, a):
+            j, gate = order[n]
+            row_tile = j * GATES + gate
+            transpose_256_rows((wx_words[:, row_tile], wh_words[:, row_tile]), grouped, a)
 
-        operands = (
-            (wx_codes, wx_scales, x_codes, x_scales),
-            (wh_codes, wh_scales, h_codes, h_scales),
-        )
-        order = [(j, gate) for j in range(HIDDEN_TILES) for gate in GATE_ORDER]
+        def quantise_weights(first, tiles, grouped):
+            cols = slice(first * 2 * P, (first + tiles) * 2 * P)
+            nc.vector.quantize_mx(
+                out=w_codes[:, cols].bitcast(FP8X4), scales=w_scales[:, cols], in_=grouped[:, 0 : tiles * 2 * P * PACK]
+            )
+
+        def prepare_weights(first, tiles):
+            grouped = new_grouped()
+            for a in range(tiles):
+                transpose_weights(first + a, grouped, a)
+            quantise_weights(first, tiles, grouped)
 
         def project(s, n, c):
-            j, gate = order[n]
-            w_codes, w_scales, a_codes, a_scales = operands[s]
-            w_cols = slice((j * GATES + gate) * P, (j * GATES + gate + 1) * P)
+            w_cols = slice((n * 2 + s) * P, (n * 2 + s + 1) * P)
+            words, codes, scales = activations[s]
             z = psum.tile([P, CHUNK], F32, tag="bank")
             nc.tensor.matmul_mx(
                 out=z[:],
                 lhsT=w_codes[:, w_cols].bitcast(FP8X4),
                 lhsT_scale=w_scales[:, w_cols],
-                rhs=a_codes[:, chunk_cols(c)].bitcast(FP8X4),
-                rhs_scale=a_scales[:, chunk_cols(c)],
+                rhs=codes[:, chunk_cols(c)].bitcast(FP8X4),
+                rhs_scale=scales[:, chunk_cols(c)],
                 start=True,
                 stop=True,
             )
             return z
 
-        stats = {}
+        stats = const.tile([P, GATE_TILES, 2, CHUNKS, STATS_DIM], F32)
         slopes = {}
         shifts = {}
-        norms = {}
-        others = {}
+        norms_h = {}
+        norms_x = {}
         values = {}
 
         def chunk_statistics(s, n, c):
             z = project(s, n, c)
-            nc.vector.bn_stats(out=stats[n][:, s, c, :], in_=z[:])
+            nc.vector.bn_stats(out=stats[:, n, s, c, :], in_=z[:])
 
-        def coefficients(n):
-            j, gate = order[n]
+        def coefficients(first, tiles):
+            mean_var = small.tile([P, tiles, 2, 2], F32, tag="mean_var%d" % tiles)
+            for k in range(tiles):
+                for s in range(2):
+                    nc.vector.bn_aggr(
+                        out=mean_var[:, k, s, :], in_=stats[:, first + k, s, :, :].rearrange("p c v -> p (c v)")
+                    )
+            j, gate = order[first]
             t = gate * HIDDEN_TILES + j
-            mean_var = small.tile([P, 2, 2], F32, tag="mean_var")
-            for s in range(2):
-                nc.vector.bn_aggr(out=mean_var[:, s, :], in_=stats[n][:, s, :, :].rearrange("p c k -> p (c k)"))
-            rstd = small.tile([P, 2], F32, tag="rstd")
+            here = slice(t, t + (tiles - 1) * 2 * HIDDEN_TILES + 1, 2 * HIDDEN_TILES)
+            gains = par[:, 0:2, here].rearrange("p s k -> p k s")
+            biases = par[:, 2:4, here].rearrange("p s k -> p k s")
+            rstd = small.tile([P, tiles, 2], F32, tag="rstd%d" % tiles)
             nc.gpsimd.tensor_scalar(
-                out=rstd[:], in0=mean_var[:, :, 1], scalar1=1.0, scalar2=EPS, op0=ALU.mult, op1=ALU.add
+                out=rstd[:], in0=mean_var[:, :, :, 1], scalar1=1.0, scalar2=EPS, op0=ALU.mult, op1=ALU.add
             )
-            nc.gpsimd.tensor_tensor(out=rstd[:], in0=rstd[:], in1=minus_half[:], op=ALU.pow)
-            slope = small.tile([P, 2], F32, tag="slope")
-            nc.gpsimd.tensor_tensor(out=slope[:], in0=rstd[:], in1=par[:, 0:2, t], op=ALU.mult)
-            shift = small.tile([P, 3], F32, tag="shift")
-            nc.gpsimd.tensor_tensor(out=shift[:, 0:2], in0=mean_var[:, :, 0], in1=slope[:], op=ALU.mult)
-            nc.gpsimd.tensor_tensor(out=shift[:, 0:2], in0=par[:, 2:4, t], in1=shift[:, 0:2], op=ALU.subtract)
-            nc.gpsimd.tensor_tensor(out=shift[:, 2:3], in0=shift[:, 0:1], in1=shift[:, 1:2], op=ALU.add)
-            slopes[n] = slope
-            shifts[n] = shift
+            nc.gpsimd.tensor_tensor(out=rstd[:], in0=rstd[:], in1=minus_half[:, 0:tiles, :], op=ALU.pow)
+            slope = small.tile([P, tiles, 2], F32, tag="slope%d" % tiles)
+            nc.gpsimd.tensor_tensor(out=slope[:], in0=rstd[:], in1=gains, op=ALU.mult)
+            part = small.tile([P, tiles, 2], F32, tag="part%d" % tiles)
+            nc.gpsimd.tensor_tensor(out=part[:], in0=mean_var[:, :, :, 0], in1=slope[:], op=ALU.mult)
+            nc.gpsimd.tensor_tensor(out=part[:], in0=biases, in1=part[:], op=ALU.subtract)
+            shift = small.tile([P, tiles, 1], F32, tag="shift%d" % tiles)
+            nc.gpsimd.tensor_tensor(out=shift[:], in0=part[:, :, 0:1], in1=part[:, :, 1:2], op=ALU.add)
+            for k in range(tiles):
+                slopes[first + k] = slope[:, k, :]
+                shifts[first + k] = shift[:, k, :]
 
-        def new_stats(n):
-            stats_n = small.tile([P, 2, CHUNKS, STATS_DIM], F32, tag="stats")
-            stats[n] = stats_n
-
-        quantise_chunk(wx_words, wx_codes, wx_scales, 0)
-        quantise_chunk(wh_words, wh_codes, wh_scales, 0)
+        prepare_weights(0, 1)
         par_bank = psum.tile([P, P], BF16, tag="bank")
         nc.tensor.transpose(par_bank[:], par_rows[:], ident_bf16[:])
         par = const.tile([P, 4, GATE_TILES], F32)
         nc.vector.tensor_copy(out=par[:].rearrange("p q t -> p (q t)"), in_=par_bank[:, 0 : 4 * GATE_TILES])
-        head_items = [divmod(i, CHUNKS) for i in range(LEAD)]
-        for n, c in head_items:
-            if c == 0:
-                new_stats(n)
-        activations = ((x_words, x_codes, x_scales), (h_words, h_codes, h_scales))
-        head_chunks = [(s, chunk) for s in range(2) for chunk in range(CHUNKS)]
+        head_chunks = [(s, c) for s in range(2) for c in range(CHUNKS)]
         for k in range(len(head_chunks) + HEAD_LAG):
             if k < len(head_chunks):
-                s, chunk = head_chunks[k]
-                quantise_chunk(*activations[s], chunk)
+                prepare_chunk(*head_chunks[k])
+            if k == len(head_chunks):
+                prepare_weights(1, 1)
             if k >= HEAD_LAG:
-                s, chunk = head_chunks[k - HEAD_LAG]
-                for n, c in head_items:
-                    if c == chunk:
-                        chunk_statistics(s, n, c)
-        for n, c in head_items:
-            if c == CHUNKS - 1:
-                coefficients(n)
+                s, c = head_chunks[k - HEAD_LAG]
+                chunk_statistics(s, 0, c)
+        coefficients(0, 1)
+        prepare_weights(2, 2)
 
         next_grouped = {}
 
         def first_sweep(i):
             n, c = divmod(i, CHUNKS)
-            if c == 0:
-                new_stats(n)
             for s in range(2):
                 chunk_statistics(s, n, c)
             if c == CHUNKS - 1:
-                coefficients(n)
+                if n == 1:
+                    coefficients(1, 1)
+                elif n % 2 == 1:
+                    coefficients(n - 1, 2)
 
         def norm_h(i):
             n, c = divmod(i, CHUNKS)
-            norm = sums.tile([P, CHUNK], F32, tag="norm")
-            norms[i] = norm
+            norm = sums.tile([P, CHUNK], F32, tag="norm_h")
+            norms_h[i] = norm
             zh = project(1, n, c)
             nc.scalar.activation(
-                out=norm[:], in_=zh[:], func=ACT.Identity, scale=slopes[n][:, 1:2], bias=shifts[n][:, 2:3]
+                out=norm[:], in_=zh[:], func=ACT.Identity, scale=slopes[n][:, 1:2], bias=shifts[n]
             )
 
         def norm_x(i):
             n, c = divmod(i, CHUNKS)
             zx = project(0, n, c)
-            if c in SPLIT:
-                other = sums.tile([P, CHUNK], F32, tag="norm_x", bufs=6)
-                nc.scalar.activation(out=other[:], in_=zx[:], func=ACT.Identity, scale=slopes[n][:, 0:1])
-                others[i] = other
-                return
-            nc.vector.scalar_tensor_tensor(
-                out=norms[i][:], in0=zx[:], scalar=slopes[n][:, 0:1], in1=norms[i][:], op0=ALU.mult, op1=ALU.add
-            )
+            if c in SPLIT_CHUNKS and i + LEAD < ITEMS:
+                norm = sums.tile([P, CHUNK], F32, tag="norm_x", bufs=4)
+                norms_x[i] = norm
+                nc.scalar.activation(out=norm[:], in_=zx[:], func=ACT.Identity, scale=slopes[n][:, 0:1])
+            else:
+                part = norms_h[i][:]
+                nc.vector.scalar_tensor_tensor(
+                    out=part, in0=zx[:], scalar=slopes[n][:, 0:1], in1=part, op0=ALU.mult, op1=ALU.add
+                )
 
         def turn(i):
             bank = psum.tile([P, TILES_PER_CHUNK, P], F32, tag="bank")
+            parts = [norms_h[i]] + ([norms_x[i]] if i in norms_x else [])
             for t in range(TILES_PER_CHUNK):
-                cols = slice(t * P, (t + 1) * P)
-                if i in others:
-                    nc.tensor.matmul(bank[:, t, :], lhsT=norms[i][:, cols], rhs=ident_f32[:], is_transpose=True, start=True, stop=False)
-                    nc.tensor.matmul(bank[:, t, :], lhsT=others[i][:, cols], rhs=ident_f32[:], is_transpose=True, start=False, stop=True)
-                else:
-                    nc.tensor.transpose(bank[:, t, :], norms[i][:, cols], ident_f32[:])
+                for k, part in enumerate(parts):
+                    nc.tensor.matmul(
+                        bank[:, t, :],
+                        lhsT=part[:, t * P : (t + 1) * P],
+                        rhs=ident_f32[:],
+                        is_transpose=True,
+                        start=k == 0,
+                        stop=k == len(parts) - 1,
+                    )
             return bank
 
         def gate_function(i, bank):
-            n, c = divmod(i, CHUNKS)
-            if c == 0:
-                value = gates.tile([P, ROW_TILES, P], F32, tag="gate")
-                values[n] = value
-            func = ACT.Tanh if order[n][1] == G_GATE else ACT.Sigmoid
-            nc.scalar.activation(out=values[n][:, chunk_tiles(c), :], in_=bank[:], func=func)
+            gate = order[i // CHUNKS][1]
+            value = gates.tile([P, TILES_PER_CHUNK, P], F32, tag="gate%d" % gate, bufs=VALUE_TILES[gate])
+            values[i] = value
+            func = ACT.Tanh if gate == G_GATE else ACT.Sigmoid
+            nc.scalar.activation(out=value[:], in_=bank[:], func=func)
 
-        def vector_is_free(n):
-            return n + VECTOR_TILES >= GATE_TILES
+        def gate_of(i):
+            return order[i // CHUNKS][1]
+
+        def candidate(i):
+            return values[i - i % (GATES * CHUNKS) + i % CHUNKS][:]
+
+        def on_vector(i):
+            return i // CHUNKS + VECTOR_TILES >= GATE_TILES
 
         def pair(i, lag):
             return [item for item in range(i - lag, i - lag + PAIR) if 0 <= item < ITEMS]
 
-        def due(i, lag, short_lag):
-            late = [item for item in pair(i, lag) if not vector_is_free(item // CHUNKS)]
-            return late + [item for item in pair(i, short_lag) if vector_is_free(item // CHUNKS)]
+        def due(i, lag, short_lag, gate):
+            late = [item for item in pair(i, lag) if not on_vector(item)]
+            early = [item for item in pair(i, short_lag) if on_vector(item)]
+            return [item for item in late + early if gate_of(item) == gate]
 
-        def products_engine(n):
-            return nc.vector if vector_is_free(n) else nc.gpsimd
+        def multiply(i, out, in0, in1, op=ALU.mult):
+            engine = nc.vector if on_vector(i) else nc.gpsimd
+            engine.tensor_tensor(out=out, in0=in0, in1=in1, op=op)
 
-        def first_product(i):
+        def store(i, out):
             n, c = divmod(i, CHUNKS)
-            j, gate = order[n]
-            mine = values[n][:, chunk_tiles(c), :]
-            if gate == I_GATE:
-                candidate = values[j * GATES][:, chunk_tiles(c), :]
-                products_engine(n).tensor_tensor(out=candidate, in0=mine, in1=candidate, op=ALU.mult)
-            if gate == F_GATE:
-                cell = c_sb[:, chunk_tiles(c), j * P : (j + 1) * P]
-                products_engine(n).tensor_tensor(out=mine, in0=mine, in1=cell, op=ALU.mult)
-
-        def second_product(i):
-            n, c = divmod(i, CHUNKS)
-            j, gate = order[n]
-            if gate != F_GATE and gate != O_GATE:
-                return
-            mine = values[n][:, chunk_tiles(c), :]
-            candidate = values[j * GATES][:, chunk_tiles(c), :]
-            op, out = (ALU.add, out_1) if gate == F_GATE else (ALU.mult, out_0)
-            products_engine(n).tensor_tensor(out=mine, in0=mine, in1=candidate, op=op)
+            j = order[n][0]
             out_rows = out.rearrange("(p t) k -> p t k", t=ROW_TILES)
-            nc.sync.dma_start(out=out_rows[:, chunk_tiles(c), j * P : (j + 1) * P], in_=mine)
-
-        def cell_tanh(i):
-            n, c = divmod(i, CHUNKS)
-            j, gate = order[n]
-            if gate == F_GATE:
-                nc.scalar.activation(
-                    out=values[j * GATES][:, chunk_tiles(c), :], in_=values[n][:, chunk_tiles(c), :], func=ACT.Tanh
-                )
+            nc.sync.dma_start(out=out_rows[:, chunk_tiles(c), j * P : (j + 1) * P], in_=values[i][:])
 
         def prepare(i):
             n, c = divmod(i, CHUNKS)
             j, gate = order[n]
             if j + 1 == HIDDEN_TILES:
                 return
-            if gate == G_GATE:
-                s, a = divmod(c, 2)
+            first = (j + 1) * GATES
+            half, a = divmod(c, 2)
+            if gate == I_GATE:
                 if a == 0:
-                    next_grouped[s] = new_grouped()
-                transpose_256_rows((wx_words, wh_words)[s], j + 1, a, next_grouped[s])
-            if gate == I_GATE and c == 0:
-                quantise(next_grouped[0], wx_codes, wx_scales, j + 1)
-                quantise(next_grouped[1], wh_codes, wh_scales, j + 1)
+                    next_grouped[half] = new_grouped()
+                transpose_weights(first + c, next_grouped[half], a)
+            if gate == G_GATE and half == 0:
+                quantise_weights(first + 2 * c, 2, next_grouped[c])
 
-        for i in range(0, ITEMS + LAST_LAG, PAIR):
+        for i in range(CHUNKS - LEAD, ITEMS + LAST_LAG, PAIR):
             turned = [(item, turn(item)) for item in pair(i, LAG_TURN)]
             for item, bank in turned:
                 gate_function(item, bank)
             for item in pair(i, 0):
                 prepare(item)
             for k in range(PAIR):
-                if i + k - LAG_NORM_X in range(ITEMS):
-                    norm_x(i + k - LAG_NORM_X)
-                if i + k + LEAD < ITEMS:
+                for item in pair(i, LAG_NORM_X)[k : k + 1]:
+                    norm_x(item)
+                if CHUNKS <= i + k + LEAD < ITEMS:
                     first_sweep(i + k + LEAD)
-                if i + k < ITEMS:
-                    norm_h(i + k)
-            for item in due(i, LAG_FIRST_PRODUCT, SHORT_PRODUCT):
-                first_product(item)
-            for item in due(i, LAG_SECOND_PRODUCT, SHORT_PRODUCT):
-                second_product(item)
-            for item in due(i, LAG_TANH, SHORT_TANH):
-                cell_tanh(item)
+                for item in pair(i, 0)[k : k + 1]:
+                    norm_h(item)
+            for item in due(i, LAG_CANDIDATE, SHORT_PRODUCT, G_GATE):
+                multiply(item, candidate(item), values[item][:], candidate(item))
+            for item in due(i, LAG_CANDIDATE, SHORT_PRODUCT, F_GATE):
+                j, c = order[item // CHUNKS][0], item % CHUNKS
+                multiply(item, values[item][:], values[item][:], c_sb[:, chunk_tiles(c), j * P : (j + 1) * P])
+            for item in due(i, LAG_CELL, SHORT_PRODUCT, F_GATE):
+                multiply(item, values[item][:], values[item][:], candidate(item), op=ALU.add)
+                store(item, out_1)
+            for item in due(i, LAG_TANH, SHORT_TANH, F_GATE):
+                nc.scalar.activation(out=candidate(item), in_=values[item][:], func=ACT.Tanh)
+            for item in due(i, LAG_HIDDEN, SHORT_PRODUCT, O_GATE):
+                multiply(item, values[item][:], values[item][:], candidate(item))
+                store(item, out_0)

@@ -39,9 +39,10 @@ PAIR = 2
 LEAD = 10
 HEAD_LAG = 2
 SPLIT_CHUNKS = (1, 3)
+SPLIT_EVERY = 2
 VECTOR_TILES = 2
 LAG_NORM_X = 2
-LAG_TURN = 4
+LAG_TURN = 6
 LAG_CANDIDATE = LAG_TURN
 LAG_CELL = LAG_TURN + 4
 LAG_TANH = LAG_TURN + 8
@@ -61,7 +62,7 @@ def tile_cleanlstm_pa_kernel(tc, x, y, h_prev, c_prev, Wx, Wh, gx, bx, gh, bh, o
         keep = ctx.enter_context(tc.tile_pool(name="keep", bufs=1))
         stage = ctx.enter_context(tc.tile_pool(name="stage", bufs=4))
         small = ctx.enter_context(tc.tile_pool(name="small", bufs=4))
-        sums = ctx.enter_context(tc.tile_pool(name="sums", bufs=8))
+        sums = ctx.enter_context(tc.tile_pool(name="sums", bufs=10))
         gates = ctx.enter_context(tc.tile_pool(name="gates", bufs=8))
         psum = ctx.enter_context(tc.psum_pool(name="psum", bufs=8))
 
@@ -273,8 +274,8 @@ def tile_cleanlstm_pa_kernel(tc, x, y, h_prev, c_prev, Wx, Wh, gx, bx, gh, bh, o
         def norm_x(i):
             n, c = divmod(i, CHUNKS)
             zx = project(0, n, c)
-            if c in SPLIT_CHUNKS and i + LEAD < ITEMS:
-                norm = sums.tile([P, CHUNK], F32, tag="norm_x", bufs=4)
+            if c in SPLIT_CHUNKS and n % SPLIT_EVERY == 0 and i + LEAD < ITEMS:
+                norm = sums.tile([P, CHUNK], F32, tag="norm_x", bufs=5)
                 norms_x[i] = norm
                 nc.scalar.activation(out=norm[:], in_=zx[:], func=ACT.Identity, scale=slopes[n][:, 0:1])
             else:

@@ -32,25 +32,33 @@ STATS_DIM = 6
 
 FLOPS = 2 * 2 * BATCH * GATES * HIDDEN * FEATURES
 
-GATE_ORDER = (I_GATE, G_GATE, F_GATE, O_GATE)
+GATE_ORDER = (F_GATE, I_GATE, G_GATE, O_GATE)
+KEPT_GATES = (I_GATE, G_GATE)
 
 ITEMS = GATE_TILES * CHUNKS
 PAIR = 2
-LEAD = 10
+LEAD = 12
+LAG_KEPT_STATISTICS = 2
+LAG_COEFFICIENTS = 4
 HEAD_LAG = 2
-SPLIT_CHUNKS = (1, 3)
-SPLIT_EVERY = 2
-VECTOR_TILES = 2
+SQUARES_FIRST = 3
+SQUARES = 1
+SPLIT_CHUNK = 3
 LAG_NORM_X = 2
 LAG_TURN = 6
-LAG_CANDIDATE = LAG_TURN
-LAG_CELL = LAG_TURN + 4
-LAG_TANH = LAG_TURN + 8
-LAG_HIDDEN = LAG_TURN + 6
-SHORT_PRODUCT = LAG_TURN
-SHORT_TANH = LAG_TURN + 2
-LAST_LAG = LAG_TANH
-VALUE_TILES = {I_GATE: 8, G_GATE: 4, F_GATE: 6, O_GATE: 6}
+LAG_FUNCTION = LAG_NORM_X + 2
+LAG_FORGET = LAG_TURN + 2
+LAG_CANDIDATE = LAG_FUNCTION
+LAG_CELL = LAG_CANDIDATE + 6
+LAG_TANH = LAG_CELL + 2
+LAG_HIDDEN = LAG_TURN + 4
+SPREAD = 1
+LATE_ITEMS = 8
+SHORT_CELL = LAG_CANDIDATE + 4
+SHORT_HIDDEN = LAG_TURN
+VECTOR_FORGET, VECTOR_CANDIDATE, VECTOR_HIDDEN = 12, 14, 15
+LAST_LAG = LAG_TANH + SPREAD * (CHUNKS - 1)
+VALUE_TILES = {F_GATE: 7, I_GATE: 5, G_GATE: 7, O_GATE: 5}
 
 
 def tile_cleanlstm_pa_kernel(tc, x, y, h_prev, c_prev, Wx, Wh, gx, bx, gh, bh, out_0, out_1):
@@ -60,9 +68,9 @@ def tile_cleanlstm_pa_kernel(tc, x, y, h_prev, c_prev, Wx, Wh, gx, bx, gh, bh, o
         const = ctx.enter_context(tc.tile_pool(name="const", bufs=1))
         raw = ctx.enter_context(tc.tile_pool(name="raw", bufs=1))
         keep = ctx.enter_context(tc.tile_pool(name="keep", bufs=1))
-        stage = ctx.enter_context(tc.tile_pool(name="stage", bufs=4))
-        small = ctx.enter_context(tc.tile_pool(name="small", bufs=4))
-        sums = ctx.enter_context(tc.tile_pool(name="sums", bufs=10))
+        stage = ctx.enter_context(tc.tile_pool(name="stage", bufs=3))
+        small = ctx.enter_context(tc.tile_pool(name="small", bufs=6))
+        sums = ctx.enter_context(tc.tile_pool(name="sums", bufs=8))
         gates = ctx.enter_context(tc.tile_pool(name="gates", bufs=8))
         psum = ctx.enter_context(tc.psum_pool(name="psum", bufs=8))
 
@@ -120,7 +128,7 @@ def tile_cleanlstm_pa_kernel(tc, x, y, h_prev, c_prev, Wx, Wh, gx, bx, gh, bh, o
         make_identity(nc, ident_f32[:])
         ident_bf16 = const.tile([P, P], BF16)
         make_identity(nc, ident_bf16[:])
-        minus_half = const.tile([P, 2, 2], F32)
+        minus_half = const.tile([P, 2], F32)
         nc.gpsimd.memset(minus_half[:], -0.5)
 
         nc.vector.tensor_copy(out=x_rows[:, :, X_WHOLE_BLOCKS : FEATURES - 1], in_=x_tail[:, :, 0:n_tail])
@@ -194,50 +202,116 @@ def tile_cleanlstm_pa_kernel(tc, x, y, h_prev, c_prev, Wx, Wh, gx, bx, gh, bh, o
             )
             return z
 
-        stats = const.tile([P, GATE_TILES, 2, CHUNKS, STATS_DIM], F32)
+        def gate_of(i):
+            return order[i // CHUNKS][1]
+
+        def is_kept(i):
+            return gate_of(i) in KEPT_GATES
+
+        def squares(n):
+            if order[n][1] not in KEPT_GATES:
+                return 0
+            return SQUARES_FIRST if n < GATES else SQUARES
+
+        def squared(i):
+            return i % CHUNKS < squares(i // CHUNKS)
+
+        stats_x = const.tile([P, GATE_TILES, CHUNKS * STATS_DIM], F32)
+        stats_h = const.tile([P, GATE_TILES, CHUNKS * STATS_DIM], F32)
+
+        def place(i):
+            n, c = divmod(i, CHUNKS)
+            if squared(i):
+                return slice(c * 3, c * 3 + 3)
+            first = squares(n) * 3 + (c - squares(n)) * STATS_DIM
+            return slice(first, first + STATS_DIM)
+
+        for i in range(ITEMS):
+            if squared(i):
+                first = place(i).start
+                nc.vector.memset(stats_h[:, i // CHUNKS, first : first + 1], float(CHUNK))
+        chunk_sums = const.tile([P, ITEMS], F32)
+        unread = const.tile([P, CHUNK], F32)
+
         slopes = {}
         shifts = {}
-        norms_h = {}
+        ratios = {}
+        sum_tiles = {}
         norms_x = {}
         values = {}
 
-        def chunk_statistics(s, n, c):
-            z = project(s, n, c)
-            nc.vector.bn_stats(out=stats[:, n, s, c, :], in_=z[:])
+        def statistics_x(i):
+            n, c = divmod(i, CHUNKS)
+            z = project(0, n, c)
+            nc.vector.bn_stats(out=stats_x[:, n, c * STATS_DIM : (c + 1) * STATS_DIM], in_=z[:])
 
-        def coefficients(first, tiles):
-            mean_var = small.tile([P, tiles, 2, 2], F32, tag="mean_var%d" % tiles)
-            for k in range(tiles):
-                for s in range(2):
-                    nc.vector.bn_aggr(
-                        out=mean_var[:, k, s, :], in_=stats[:, first + k, s, :, :].rearrange("p c v -> p (c v)")
-                    )
-            j, gate = order[first]
-            t = gate * HIDDEN_TILES + j
-            here = slice(t, t + (tiles - 1) * 2 * HIDDEN_TILES + 1, 2 * HIDDEN_TILES)
-            gains = par[:, 0:2, here].rearrange("p s k -> p k s")
-            biases = par[:, 2:4, here].rearrange("p s k -> p k s")
-            rstd = small.tile([P, tiles, 2], F32, tag="rstd%d" % tiles)
-            nc.gpsimd.tensor_scalar(
-                out=rstd[:], in0=mean_var[:, :, :, 1], scalar1=1.0, scalar2=EPS, op0=ALU.mult, op1=ALU.add
+        def take_h(i):
+            n, c = divmod(i, CHUNKS)
+            z = project(1, n, c)
+            if not is_kept(i):
+                nc.vector.bn_stats(out=stats_h[:, n, place(i)], in_=z[:])
+                return
+            kept = sums.tile([P, CHUNK], F32, tag="kept", bufs=10)
+            sum_tiles[i] = kept
+            if squared(i):
+                nc.scalar.activation(out=kept[:], in_=z[:], func=ACT.Identity, accum_out=chunk_sums[:, i : i + 1])
+            else:
+                nc.scalar.copy(out=kept[:], in_=z[:])
+
+        def kept_statistics(i):
+            if not is_kept(i):
+                return
+            n = i // CHUNKS
+            if not squared(i):
+                nc.vector.bn_stats(out=stats_h[:, n, place(i)], in_=sum_tiles[i][:])
+                return
+            first = place(i).start
+            mean = stats_h[:, n, first + 1 : first + 2]
+            nc.scalar.mul(out=mean, in_=chunk_sums[:, i : i + 1], mul=1.0 / CHUNK)
+            nc.scalar.activation(
+                out=unread[:],
+                in_=sum_tiles[i][:],
+                func=ACT.Square,
+                scale=-1.0,
+                bias=mean,
+                accum_out=stats_h[:, n, first + 2 : first + 3],
             )
-            nc.gpsimd.tensor_tensor(out=rstd[:], in0=rstd[:], in1=minus_half[:, 0:tiles, :], op=ALU.pow)
-            slope = small.tile([P, tiles, 2], F32, tag="slope%d" % tiles)
-            nc.gpsimd.tensor_tensor(out=slope[:], in0=rstd[:], in1=gains, op=ALU.mult)
-            part = small.tile([P, tiles, 2], F32, tag="part%d" % tiles)
-            nc.gpsimd.tensor_tensor(out=part[:], in0=mean_var[:, :, :, 0], in1=slope[:], op=ALU.mult)
-            nc.gpsimd.tensor_tensor(out=part[:], in0=biases, in1=part[:], op=ALU.subtract)
-            shift = small.tile([P, tiles, 1], F32, tag="shift%d" % tiles)
-            nc.gpsimd.tensor_tensor(out=shift[:], in0=part[:, :, 0:1], in1=part[:, :, 1:2], op=ALU.add)
-            for k in range(tiles):
-                slopes[first + k] = slope[:, k, :]
-                shifts[first + k] = shift[:, k, :]
+
+        def coefficients(n):
+            mean_var = small.tile([P, 2, 2], F32, tag="mean_var")
+            nc.vector.bn_aggr(out=mean_var[:, 0, :], in_=stats_x[:, n, :])
+            nc.vector.bn_aggr(out=mean_var[:, 1, :], in_=stats_h[:, n, 0 : place(n * CHUNKS + CHUNKS - 1).stop])
+            j, gate = order[n]
+            t = gate * HIDDEN_TILES + j
+            var = small.tile([P, 2], F32, tag="var")
+            nc.gpsimd.tensor_scalar(
+                out=var[:], in0=mean_var[:, :, 1], scalar1=1.0, scalar2=EPS, op0=ALU.mult, op1=ALU.add
+            )
+            rstd = small.tile([P, 2], F32, tag="rstd")
+            nc.gpsimd.tensor_tensor(out=rstd[:], in0=var[:], in1=minus_half[:], op=ALU.pow)
+            slope = small.tile([P, 2], F32, tag="slope")
+            nc.gpsimd.tensor_tensor(out=slope[:], in0=rstd[:], in1=par[:, 0:2, t], op=ALU.mult)
+            if gate in KEPT_GATES:
+                ratio = small.tile([P, 2], F32, tag="ratio")
+                nc.gpsimd.tensor_scalar(
+                    out=ratio[:, 0:1],
+                    in0=rstd[:, 1:2],
+                    scalar1=var[:, 1:2],
+                    scalar2=inverse_gain[:, t : t + 1],
+                    op0=ALU.mult,
+                    op1=ALU.mult,
+                )
+                nc.gpsimd.tensor_tensor(out=ratio[:, 1:2], in0=ratio[:, 0:1], in1=slope[:, 0:1], op=ALU.mult)
+                ratios[n] = ratio[:, 1:2]
+            part = small.tile([P, 2], F32, tag="part")
+            nc.gpsimd.tensor_tensor(out=part[:], in0=mean_var[:, :, 0], in1=slope[:], op=ALU.mult)
+            nc.gpsimd.tensor_tensor(out=part[:], in0=par[:, 2:4, t], in1=part[:], op=ALU.subtract)
+            shift = small.tile([P, 1], F32, tag="shift")
+            nc.gpsimd.tensor_tensor(out=shift[:], in0=part[:, 0:1], in1=part[:, 1:2], op=ALU.add)
+            slopes[n] = slope
+            shifts[n] = shift
 
         prepare_weights(0, 1)
-        par_bank = psum.tile([P, P], BF16, tag="bank")
-        nc.tensor.transpose(par_bank[:], par_rows[:], ident_bf16[:])
-        par = const.tile([P, 4, GATE_TILES], F32)
-        nc.vector.tensor_copy(out=par[:].rearrange("p q t -> p (q t)"), in_=par_bank[:, 0 : 4 * GATE_TILES])
         head_chunks = [(s, c) for s in range(2) for c in range(CHUNKS)]
         for k in range(len(head_chunks) + HEAD_LAG):
             if k < len(head_chunks):
@@ -246,47 +320,48 @@ def tile_cleanlstm_pa_kernel(tc, x, y, h_prev, c_prev, Wx, Wh, gx, bx, gh, bh, o
                 prepare_weights(1, 1)
             if k >= HEAD_LAG:
                 s, c = head_chunks[k - HEAD_LAG]
-                chunk_statistics(s, 0, c)
-        coefficients(0, 1)
+                (statistics_x, take_h)[s](c)
+        par_bank = psum.tile([P, P], BF16, tag="bank")
+        nc.tensor.transpose(par_bank[:], par_rows[:], ident_bf16[:])
+        par = const.tile([P, 4, GATE_TILES], F32)
+        nc.vector.tensor_copy(out=par[:].rearrange("p q t -> p (q t)"), in_=par_bank[:, 0 : 4 * GATE_TILES])
+        gain_h = par[:, 1, :]
+        more = const.tile([P, GATE_TILES], F32)
+        nc.vector.scalar_tensor_tensor(out=more[:], in0=gain_h, scalar=-1.0, in1=gain_h, op0=ALU.mult, op1=ALU.max)
+        nc.vector.tensor_scalar(out=more[:], in0=more[:], scalar1=2e-18, scalar2=4e-18, op0=ALU.is_lt, op1=ALU.mult)
+        nc.vector.tensor_tensor(out=gain_h, in0=gain_h, in1=more[:], op=ALU.add)
+        inverse_gain = const.tile([P, GATE_TILES], F32)
+        nc.vector.reciprocal(out=inverse_gain[:], in_=gain_h)
+        coefficients(0)
         prepare_weights(2, 2)
 
         next_grouped = {}
 
-        def first_sweep(i):
-            n, c = divmod(i, CHUNKS)
-            for s in range(2):
-                chunk_statistics(s, n, c)
-            if c == CHUNKS - 1:
-                if n == 1:
-                    coefficients(1, 1)
-                elif n % 2 == 1:
-                    coefficients(n - 1, 2)
-
         def norm_h(i):
             n, c = divmod(i, CHUNKS)
             norm = sums.tile([P, CHUNK], F32, tag="norm_h")
-            norms_h[i] = norm
+            sum_tiles[i] = norm
             zh = project(1, n, c)
             nc.scalar.activation(
-                out=norm[:], in_=zh[:], func=ACT.Identity, scale=slopes[n][:, 1:2], bias=shifts[n]
+                out=norm[:], in_=zh[:], func=ACT.Identity, scale=slopes[n][:, 1:2], bias=shifts[n][:]
             )
 
-        def norm_x(i):
+        def add_x(i):
             n, c = divmod(i, CHUNKS)
             zx = project(0, n, c)
-            if c in SPLIT_CHUNKS and n % SPLIT_EVERY == 0 and i + LEAD < ITEMS:
-                norm = sums.tile([P, CHUNK], F32, tag="norm_x", bufs=5)
+            if not is_kept(i) and c == SPLIT_CHUNK and not is_late(i):
+                norm = sums.tile([P, CHUNK], F32, tag="norm_x", bufs=4)
                 norms_x[i] = norm
                 nc.scalar.activation(out=norm[:], in_=zx[:], func=ACT.Identity, scale=slopes[n][:, 0:1])
             else:
-                part = norms_h[i][:]
+                part = sum_tiles[i][:]
+                factor = ratios[n] if is_kept(i) else slopes[n][:, 0:1]
                 nc.vector.scalar_tensor_tensor(
-                    out=part, in0=zx[:], scalar=slopes[n][:, 0:1], in1=part, op0=ALU.mult, op1=ALU.add
+                    out=part, in0=zx[:], scalar=factor, in1=part, op0=ALU.mult, op1=ALU.add
                 )
 
-        def turn(i):
+        def turn(*parts):
             bank = psum.tile([P, TILES_PER_CHUNK, P], F32, tag="bank")
-            parts = [norms_h[i]] + ([norms_x[i]] if i in norms_x else [])
             for t in range(TILES_PER_CHUNK):
                 for k, part in enumerate(parts):
                     nc.tensor.matmul(
@@ -299,77 +374,111 @@ def tile_cleanlstm_pa_kernel(tc, x, y, h_prev, c_prev, Wx, Wh, gx, bx, gh, bh, o
                     )
             return bank
 
-        def gate_function(i, bank):
-            gate = order[i // CHUNKS][1]
-            value = gates.tile([P, TILES_PER_CHUNK, P], F32, tag="gate%d" % gate, bufs=VALUE_TILES[gate])
+        def new_value(i):
+            gate = gate_of(i)
+            value = gates.tile([P, CHUNK], F32, tag="gate%d" % gate, bufs=VALUE_TILES[gate])
             values[i] = value
-            func = ACT.Tanh if gate == G_GATE else ACT.Sigmoid
-            nc.scalar.activation(out=value[:], in_=bank[:], func=func)
+            return value
 
-        def gate_of(i):
-            return order[i // CHUNKS][1]
+        def by_row_tile(ap):
+            return ap.rearrange("p (t f) -> p t f", t=TILES_PER_CHUNK)
 
-        def candidate(i):
-            return values[i - i % (GATES * CHUNKS) + i % CHUNKS][:]
+        def turned_function(i, bank):
+            nc.scalar.activation(out=by_row_tile(new_value(i)[:]), in_=bank[:], func=ACT.Sigmoid)
 
-        def on_vector(i):
-            return i // CHUNKS + VECTOR_TILES >= GATE_TILES
+        def gate_function(i):
+            n = i // CHUNKS
+            func = ACT.Tanh if gate_of(i) == G_GATE else ACT.Sigmoid
+            nc.scalar.activation(
+                out=new_value(i)[:], in_=sum_tiles[i][:], func=func, scale=slopes[n][:, 1:2], bias=shifts[n][:]
+            )
+
+        def is_late(i):
+            return i + LATE_ITEMS >= ITEMS
 
         def pair(i, lag):
             return [item for item in range(i - lag, i - lag + PAIR) if 0 <= item < ITEMS]
 
-        def due(i, lag, short_lag, gate):
-            late = [item for item in pair(i, lag) if not on_vector(item)]
-            early = [item for item in pair(i, short_lag) if on_vector(item)]
-            return [item for item in late + early if gate_of(item) == gate]
-
-        def multiply(i, out, in0, in1, op=ALU.mult):
-            engine = nc.vector if on_vector(i) else nc.gpsimd
-            engine.tensor_tensor(out=out, in0=in0, in1=in1, op=op)
+        def due(i, gate, lag, short_lag, spread):
+            items = []
+            for item in range(ITEMS):
+                if gate_of(item) == gate:
+                    when = item + (short_lag if is_late(item) else lag + spread * (item % CHUNKS))
+                    if i <= when < i + PAIR:
+                        items.append(item)
+            return items
 
         def store(i, out):
             n, c = divmod(i, CHUNKS)
             j = order[n][0]
             out_rows = out.rearrange("(p t) k -> p t k", t=ROW_TILES)
-            nc.sync.dma_start(out=out_rows[:, chunk_tiles(c), j * P : (j + 1) * P], in_=values[i][:])
+            nc.sync.dma_start(
+                out=out_rows[:, chunk_tiles(c), j * P : (j + 1) * P], in_=by_row_tile(values[i][:])
+            )
 
         def prepare(i):
             n, c = divmod(i, CHUNKS)
-            j, gate = order[n]
-            if j + 1 == HIDDEN_TILES:
+            if n + GATES >= GATE_TILES:
                 return
-            first = (j + 1) * GATES
-            half, a = divmod(c, 2)
-            if gate == I_GATE:
-                if a == 0:
-                    next_grouped[half] = new_grouped()
-                transpose_weights(first + c, next_grouped[half], a)
-            if gate == G_GATE and half == 0:
-                quantise_weights(first + 2 * c, 2, next_grouped[c])
+            if c == 0:
+                next_grouped[n] = new_grouped()
+                transpose_weights(n + GATES, next_grouped[n], 0)
+            if c == 2:
+                quantise_weights(n + GATES, 1, next_grouped[n])
+
+        def engine_from(first_tile, i):
+            return nc.vector if i // CHUNKS >= first_tile else nc.gpsimd
 
         for i in range(CHUNKS - LEAD, ITEMS + LAST_LAG, PAIR):
-            turned = [(item, turn(item)) for item in pair(i, LAG_TURN)]
+            turned = []
+            for gate in (F_GATE, O_GATE):
+                for item in pair(i, LAG_TURN):
+                    if gate_of(item) == gate:
+                        parts = [sum_tiles[item]] + ([norms_x[item]] if item in norms_x else [])
+                        turned.append((item, turn(*parts)))
+            cells = [(item, turn(values[item])) for item in due(i, G_GATE, LAG_CELL, SHORT_CELL, SPREAD)]
             for item, bank in turned:
-                gate_function(item, bank)
+                turned_function(item, bank)
+            for item, bank in cells:
+                forget = item - 2 * CHUNKS
+                cell = by_row_tile(values[forget][:])
+                nc.vector.tensor_tensor(out=cell, in0=bank[:], in1=cell, op=ALU.add)
+                store(forget, out_1)
             for item in pair(i, 0):
                 prepare(item)
             for k in range(PAIR):
                 for item in pair(i, LAG_NORM_X)[k : k + 1]:
-                    norm_x(item)
-                if CHUNKS <= i + k + LEAD < ITEMS:
-                    first_sweep(i + k + LEAD)
+                    add_x(item)
+                ahead = i + k + LEAD
+                if CHUNKS <= ahead < ITEMS:
+                    statistics_x(ahead)
+                    take_h(ahead)
+                if CHUNKS <= ahead - LAG_KEPT_STATISTICS < ITEMS:
+                    kept_statistics(ahead - LAG_KEPT_STATISTICS)
+                n, c = divmod(ahead - LAG_COEFFICIENTS, CHUNKS)
+                if 1 <= n < GATE_TILES and c == CHUNKS - 1:
+                    coefficients(n)
                 for item in pair(i, 0)[k : k + 1]:
-                    norm_h(item)
-            for item in due(i, LAG_CANDIDATE, SHORT_PRODUCT, G_GATE):
-                multiply(item, candidate(item), values[item][:], candidate(item))
-            for item in due(i, LAG_CANDIDATE, SHORT_PRODUCT, F_GATE):
+                    if not is_kept(item):
+                        norm_h(item)
+                for item in pair(i, LAG_FUNCTION)[k : k + 1]:
+                    if is_kept(item):
+                        gate_function(item)
+            for item in due(i, G_GATE, LAG_TANH, SHORT_CELL + 2, SPREAD):
+                nc.scalar.activation(out=values[item][:], in_=values[item - 2 * CHUNKS][:], func=ACT.Tanh)
+            for item in due(i, F_GATE, LAG_FORGET, LAG_FORGET, 0):
                 j, c = order[item // CHUNKS][0], item % CHUNKS
-                multiply(item, values[item][:], values[item][:], c_sb[:, chunk_tiles(c), j * P : (j + 1) * P])
-            for item in due(i, LAG_CELL, SHORT_PRODUCT, F_GATE):
-                multiply(item, values[item][:], values[item][:], candidate(item), op=ALU.add)
-                store(item, out_1)
-            for item in due(i, LAG_TANH, SHORT_TANH, F_GATE):
-                nc.scalar.activation(out=candidate(item), in_=values[item][:], func=ACT.Tanh)
-            for item in due(i, LAG_HIDDEN, SHORT_PRODUCT, O_GATE):
-                multiply(item, values[item][:], values[item][:], candidate(item))
+                mine = by_row_tile(values[item][:])
+                cell = c_sb[:, chunk_tiles(c), j * P : (j + 1) * P]
+                engine_from(VECTOR_FORGET, item).tensor_tensor(out=mine, in0=mine, in1=cell, op=ALU.mult)
+            for item in due(i, G_GATE, LAG_CANDIDATE, LAG_CANDIDATE, 0):
+                mine = values[item][:]
+                engine_from(VECTOR_CANDIDATE, item).tensor_tensor(
+                    out=mine, in0=values[item - CHUNKS][:], in1=mine, op=ALU.mult
+                )
+            for item in due(i, O_GATE, LAG_HIDDEN, SHORT_HIDDEN, SPREAD):
+                mine = values[item][:]
+                engine_from(VECTOR_HIDDEN, item).tensor_tensor(
+                    out=mine, in0=mine, in1=values[item - CHUNKS][:], op=ALU.mult
+                )
                 store(item, out_0)

@@ -32,33 +32,34 @@ STATS_DIM = 6
 
 FLOPS = 2 * 2 * BATCH * GATES * HIDDEN * FEATURES
 
-GATE_ORDER = (F_GATE, I_GATE, G_GATE, O_GATE)
+GATE_ORDER = (F_GATE, I_GATE, O_GATE, G_GATE)
 KEPT_GATES = (I_GATE, G_GATE)
-
-ITEMS = GATE_TILES * CHUNKS
 PAIR = 2
-LEAD = 12
-LAG_KEPT_STATISTICS = 2
-LAG_COEFFICIENTS = 4
+ITEMS = GATE_TILES * CHUNKS
+BLOCK = PAIR * CHUNKS
+BLOCKS = ITEMS // BLOCK
+
+LEAD = BLOCK + 3 * PAIR
+LEAD_PREPARE = BLOCK
+LAG_SQUARES = PAIR
 HEAD_LAG = 2
-SQUARES_FIRST = 3
-SQUARES = 1
-SPLIT_CHUNK = 3
-LAG_NORM_X = 2
+LAG_ADD_X = 2
 LAG_TURN = 6
-LAG_FUNCTION = LAG_NORM_X + 2
+LAG_FUNCTION = LAG_ADD_X + 2
 LAG_FORGET = LAG_TURN + 2
 LAG_CANDIDATE = LAG_FUNCTION
 LAG_CELL = LAG_CANDIDATE + 6
 LAG_TANH = LAG_CELL + 2
-LAG_HIDDEN = LAG_TURN + 4
-SPREAD = 1
-LATE_ITEMS = 8
+LAG_HIDDEN = LAG_TANH + 1
 SHORT_CELL = LAG_CANDIDATE + 4
+SHORT_TANH = SHORT_CELL + 2
 SHORT_HIDDEN = LAG_TURN
-VECTOR_FORGET, VECTOR_CANDIDATE, VECTOR_HIDDEN = 12, 14, 15
-LAST_LAG = LAG_TANH + SPREAD * (CHUNKS - 1)
-VALUE_TILES = {F_GATE: 7, I_GATE: 5, G_GATE: 7, O_GATE: 5}
+VECTOR_FORGET = ITEMS - 2 * BLOCK
+VECTOR_HIDDEN = ITEMS - BLOCK
+LAST_LAG = LAG_HIDDEN
+KEPT_TILES = 12
+NORM_TILES = 5
+VALUE_TILES = {F_GATE: 9, I_GATE: 6, O_GATE: 7, G_GATE: 7}
 
 
 def tile_cleanlstm_pa_kernel(tc, x, y, h_prev, c_prev, Wx, Wh, gx, bx, gh, bh, out_0, out_1):
@@ -69,8 +70,8 @@ def tile_cleanlstm_pa_kernel(tc, x, y, h_prev, c_prev, Wx, Wh, gx, bx, gh, bh, o
         raw = ctx.enter_context(tc.tile_pool(name="raw", bufs=1))
         keep = ctx.enter_context(tc.tile_pool(name="keep", bufs=1))
         stage = ctx.enter_context(tc.tile_pool(name="stage", bufs=3))
-        small = ctx.enter_context(tc.tile_pool(name="small", bufs=6))
-        sums = ctx.enter_context(tc.tile_pool(name="sums", bufs=8))
+        small = ctx.enter_context(tc.tile_pool(name="small", bufs=4))
+        sums = ctx.enter_context(tc.tile_pool(name="sums", bufs=KEPT_TILES))
         gates = ctx.enter_context(tc.tile_pool(name="gates", bufs=8))
         psum = ctx.enter_context(tc.psum_pool(name="psum", bufs=8))
 
@@ -79,6 +80,28 @@ def tile_cleanlstm_pa_kernel(tc, x, y, h_prev, c_prev, Wx, Wh, gx, bx, gh, bh, o
 
         def chunk_tiles(c):
             return slice(c * TILES_PER_CHUNK, (c + 1) * TILES_PER_CHUNK)
+
+        order = [(j, gate) for j in range(HIDDEN_TILES) for gate in GATE_ORDER]
+
+        def tile_and_chunk(i):
+            block, rest = divmod(i, BLOCK)
+            if block == BLOCKS - 1:
+                return block * PAIR + 1 - rest // CHUNKS, rest % CHUNKS
+            return block * PAIR + rest % PAIR, rest // PAIR
+
+        item_at = {}
+        for i in range(ITEMS):
+            item_at[tile_and_chunk(i)] = i
+
+        def sibling(i, tiles):
+            n, c = tile_and_chunk(i)
+            return item_at[(n + tiles, c)]
+
+        def gate_of(i):
+            return order[tile_and_chunk(i)[0]][1]
+
+        def is_kept(i):
+            return gate_of(i) in KEPT_GATES
 
         x_sb = raw.tile([P, ROW_TILES * FEATURES], BF16)
         x_rows = x_sb[:].rearrange("p (t k) -> p t k", t=ROW_TILES)
@@ -106,17 +129,20 @@ def tile_cleanlstm_pa_kernel(tc, x, y, h_prev, c_prev, Wx, Wh, gx, bx, gh, bh, o
                 out=par_rows[q * GATE_TILES : (q + 1) * GATE_TILES, :], in_=vec.rearrange("(t p) -> t p", p=P)
             )
 
-        nc.sync.dma_start(out=wx_rows[:, 0, GATE_ORDER[0]], in_=wx_dram[:, 0, GATE_ORDER[0]])
-        nc.sync.dma_start(out=wh_rows[:, 0, GATE_ORDER[0]], in_=wh_dram[:, 0, GATE_ORDER[0]])
+        def load_weights(j, gate):
+            nc.sync.dma_start(out=wx_rows[:, j, gate], in_=wx_dram[:, j, gate])
+            nc.sync.dma_start(out=wh_rows[:, j, gate], in_=wh_dram[:, j, gate])
+
+        for gate in GATE_ORDER[0:PAIR]:
+            load_weights(0, gate)
         for c in range(CHUNKS):
             nc.sync.dma_start(
                 out=x_rows[:, chunk_tiles(c), 0:X_WHOLE_BLOCKS], in_=x_dram[:, chunk_tiles(c), 0:X_WHOLE_BLOCKS]
             )
         for c in range(CHUNKS):
             nc.sync.dma_start(out=h_rows[:, chunk_tiles(c), :], in_=h_dram[:, chunk_tiles(c), :])
-        for gate in GATE_ORDER[1:]:
-            nc.sync.dma_start(out=wx_rows[:, 0, gate], in_=wx_dram[:, 0, gate])
-            nc.sync.dma_start(out=wh_rows[:, 0, gate], in_=wh_dram[:, 0, gate])
+        for gate in GATE_ORDER[PAIR:]:
+            load_weights(0, gate)
         nc.sync.dma_start(out=wx_rows[:, 1], in_=wx_dram[:, 1])
         nc.sync.dma_start(out=wh_rows[:, 1], in_=wh_dram[:, 1])
         nc.sync.dma_start(out=c_sb[:], in_=c_prev.rearrange("(p t) k -> p t k", t=ROW_TILES))
@@ -128,7 +154,7 @@ def tile_cleanlstm_pa_kernel(tc, x, y, h_prev, c_prev, Wx, Wh, gx, bx, gh, bh, o
         make_identity(nc, ident_f32[:])
         ident_bf16 = const.tile([P, P], BF16)
         make_identity(nc, ident_bf16[:])
-        minus_half = const.tile([P, 2], F32)
+        minus_half = const.tile([P, PAIR, 2], F32)
         nc.gpsimd.memset(minus_half[:], -0.5)
 
         nc.vector.tensor_copy(out=x_rows[:, :, X_WHOLE_BLOCKS : FEATURES - 1], in_=x_tail[:, :, 0:n_tail])
@@ -146,19 +172,21 @@ def tile_cleanlstm_pa_kernel(tc, x, y, h_prev, c_prev, Wx, Wh, gx, bx, gh, bh, o
         wx_words = wx_sb[:].bitcast(F32).rearrange("p (t w) -> p t w", w=WORDS)
         wh_words = wh_sb[:].bitcast(F32).rearrange("p (t w) -> p t w", w=WORDS)
         activations = ((x_words, x_codes, x_scales), (h_words, h_codes, h_scales))
-        order = [(j, gate) for j in range(HIDDEN_TILES) for gate in GATE_ORDER]
 
         def new_grouped():
             grouped = stage.tile([P, CHUNK * PACK], BF16, tag="grouped", align_bytes=64)
             return grouped
 
-        def transpose_256_rows(blocks, grouped, a):
+        def transpose_256_rows(row_blocks, grouped, a):
             grouped_words = grouped[:].bitcast(F32).rearrange("p (a t r u) -> p a t r u", a=2, t=2, u=2)
             bank = psum.tile([P, 2, 2, P], F32, tag="bank")
-            for t, words in enumerate(blocks):
+            for t, words in enumerate(row_blocks):
                 for u in range(2):
                     nc.tensor.transpose(bank[:, t, u, :], words[:, u : 2 * P : 2], ident_f32[:])
             nc.scalar.copy(out=grouped_words[:, a], in_=bank[:].rearrange("p t u r -> p t r u"))
+
+        def quantise(grouped, codes, scales, cols):
+            nc.vector.quantize_mx(out=codes[:, cols].bitcast(FP8X4), scales=scales[:, cols], in_=grouped[:])
 
         def prepare_chunk(s, c):
             words, codes, scales = activations[s]
@@ -166,28 +194,25 @@ def tile_cleanlstm_pa_kernel(tc, x, y, h_prev, c_prev, Wx, Wh, gx, bx, gh, bh, o
             for a in range(2):
                 first = c * TILES_PER_CHUNK + 2 * a
                 transpose_256_rows((words[:, first], words[:, first + 1]), grouped, a)
-            nc.vector.quantize_mx(
-                out=codes[:, chunk_cols(c)].bitcast(FP8X4), scales=scales[:, chunk_cols(c)], in_=grouped[:]
-            )
+            quantise(grouped, codes, scales, chunk_cols(c))
 
-        def transpose_weights(n, grouped, a):
-            j, gate = order[n]
+        def transpose_weights(block, a, grouped):
+            j, gate = order[block * PAIR + a]
             row_tile = j * GATES + gate
             transpose_256_rows((wx_words[:, row_tile], wh_words[:, row_tile]), grouped, a)
 
-        def quantise_weights(first, tiles, grouped):
-            cols = slice(first * 2 * P, (first + tiles) * 2 * P)
-            nc.vector.quantize_mx(
-                out=w_codes[:, cols].bitcast(FP8X4), scales=w_scales[:, cols], in_=grouped[:, 0 : tiles * 2 * P * PACK]
-            )
+        def quantise_weights(block, grouped):
+            width = PAIR * 2 * P
+            quantise(grouped, w_codes, w_scales, slice(block * width, (block + 1) * width))
 
-        def prepare_weights(first, tiles):
+        def prepare_weights(block):
             grouped = new_grouped()
-            for a in range(tiles):
-                transpose_weights(first + a, grouped, a)
-            quantise_weights(first, tiles, grouped)
+            for a in range(PAIR):
+                transpose_weights(block, a, grouped)
+            quantise_weights(block, grouped)
 
-        def project(s, n, c):
+        def project(s, i):
+            n, c = tile_and_chunk(i)
             w_cols = slice((n * 2 + s) * P, (n * 2 + s + 1) * P)
             words, codes, scales = activations[s]
             z = psum.tile([P, CHUNK], F32, tag="bank")
@@ -202,176 +227,171 @@ def tile_cleanlstm_pa_kernel(tc, x, y, h_prev, c_prev, Wx, Wh, gx, bx, gh, bh, o
             )
             return z
 
-        def gate_of(i):
-            return order[i // CHUNKS][1]
-
-        def is_kept(i):
-            return gate_of(i) in KEPT_GATES
-
-        def squares(n):
-            if order[n][1] not in KEPT_GATES:
-                return 0
-            return SQUARES_FIRST if n < GATES else SQUARES
-
-        def squared(i):
-            return i % CHUNKS < squares(i // CHUNKS)
-
-        stats_x = const.tile([P, GATE_TILES, CHUNKS * STATS_DIM], F32)
-        stats_h = const.tile([P, GATE_TILES, CHUNKS * STATS_DIM], F32)
-
-        def place(i):
-            n, c = divmod(i, CHUNKS)
-            if squared(i):
-                return slice(c * 3, c * 3 + 3)
-            first = squares(n) * 3 + (c - squares(n)) * STATS_DIM
-            return slice(first, first + STATS_DIM)
-
-        for i in range(ITEMS):
-            if squared(i):
-                first = place(i).start
-                nc.vector.memset(stats_h[:, i // CHUNKS, first : first + 1], float(CHUNK))
-        chunk_sums = const.tile([P, ITEMS], F32)
+        stats_x = const.tile([P, GATE_TILES, CHUNKS, STATS_DIM], F32)
+        stats_h = const.tile([P, BLOCKS, CHUNKS, STATS_DIM], F32)
+        stats_kept = const.tile([P, BLOCKS, CHUNKS, 3], F32)
+        nc.vector.memset(stats_kept[:, :, :, 0:1], float(CHUNK))
+        kept_sums = const.tile([P, ITEMS], F32)
         unread = const.tile([P, CHUNK], F32)
 
         slopes = {}
         shifts = {}
         ratios = {}
         sum_tiles = {}
-        norms_x = {}
         values = {}
 
         def statistics_x(i):
-            n, c = divmod(i, CHUNKS)
-            z = project(0, n, c)
-            nc.vector.bn_stats(out=stats_x[:, n, c * STATS_DIM : (c + 1) * STATS_DIM], in_=z[:])
+            n, c = tile_and_chunk(i)
+            z = project(0, i)
+            nc.vector.bn_stats(out=stats_x[:, n, c, :], in_=z[:])
 
         def take_h(i):
-            n, c = divmod(i, CHUNKS)
-            z = project(1, n, c)
-            if not is_kept(i):
-                nc.vector.bn_stats(out=stats_h[:, n, place(i)], in_=z[:])
-                return
-            kept = sums.tile([P, CHUNK], F32, tag="kept", bufs=10)
-            sum_tiles[i] = kept
-            if squared(i):
-                nc.scalar.activation(out=kept[:], in_=z[:], func=ACT.Identity, accum_out=chunk_sums[:, i : i + 1])
+            n, c = tile_and_chunk(i)
+            z = project(1, i)
+            if is_kept(i):
+                kept = sums.tile([P, CHUNK], F32, tag="kept")
+                sum_tiles[i] = kept
+                nc.scalar.activation(out=kept[:], in_=z[:], func=ACT.Identity, accum_out=kept_sums[:, i : i + 1])
             else:
-                nc.scalar.copy(out=kept[:], in_=z[:])
+                nc.vector.bn_stats(out=stats_h[:, n // PAIR, c, :], in_=z[:])
 
-        def kept_statistics(i):
-            if not is_kept(i):
-                return
-            n = i // CHUNKS
-            if not squared(i):
-                nc.vector.bn_stats(out=stats_h[:, n, place(i)], in_=sum_tiles[i][:])
-                return
-            first = place(i).start
-            mean = stats_h[:, n, first + 1 : first + 2]
-            nc.scalar.mul(out=mean, in_=chunk_sums[:, i : i + 1], mul=1.0 / CHUNK)
+        def kept_triple(i):
+            n, c = tile_and_chunk(i)
+            return stats_kept[:, n // PAIR, c, :]
+
+        def kept_mean(i):
+            nc.scalar.mul(out=kept_triple(i)[:, 1:2], in_=kept_sums[:, i : i + 1], mul=1.0 / CHUNK)
+
+        def kept_squares(i):
+            triple = kept_triple(i)
             nc.scalar.activation(
                 out=unread[:],
                 in_=sum_tiles[i][:],
                 func=ACT.Square,
                 scale=-1.0,
-                bias=mean,
-                accum_out=stats_h[:, n, first + 2 : first + 3],
+                bias=triple[:, 1:2],
+                accum_out=triple[:, 2:3],
             )
 
-        def coefficients(n):
-            mean_var = small.tile([P, 2, 2], F32, tag="mean_var")
-            nc.vector.bn_aggr(out=mean_var[:, 0, :], in_=stats_x[:, n, :])
-            nc.vector.bn_aggr(out=mean_var[:, 1, :], in_=stats_h[:, n, 0 : place(n * CHUNKS + CHUNKS - 1).stop])
-            j, gate = order[n]
-            t = gate * HIDDEN_TILES + j
-            var = small.tile([P, 2], F32, tag="var")
+        def coefficients(block):
+            first = block * PAIR
+            here = slice(first, first + PAIR)
+            mean_var = small.tile([P, PAIR, 2, 2], F32, tag="mean_var")
+            for a, of_h in enumerate((stats_h, stats_kept)):
+                for s, triples in enumerate((stats_x[:, first + a], of_h[:, block])):
+                    nc.vector.bn_aggr(out=mean_var[:, a, s, :], in_=triples.rearrange("p c v -> p (c v)"))
+            var = small.tile([P, PAIR, 2], F32, tag="var")
             nc.gpsimd.tensor_scalar(
-                out=var[:], in0=mean_var[:, :, 1], scalar1=1.0, scalar2=EPS, op0=ALU.mult, op1=ALU.add
+                out=var[:], in0=mean_var[:, :, :, 1], scalar1=1.0, scalar2=EPS, op0=ALU.mult, op1=ALU.add
             )
-            rstd = small.tile([P, 2], F32, tag="rstd")
+            rstd = small.tile([P, PAIR, 2], F32, tag="rstd")
             nc.gpsimd.tensor_tensor(out=rstd[:], in0=var[:], in1=minus_half[:], op=ALU.pow)
-            slope = small.tile([P, 2], F32, tag="slope")
-            nc.gpsimd.tensor_tensor(out=slope[:], in0=rstd[:], in1=par[:, 0:2, t], op=ALU.mult)
-            if gate in KEPT_GATES:
-                ratio = small.tile([P, 2], F32, tag="ratio")
-                nc.gpsimd.tensor_scalar(
-                    out=ratio[:, 0:1],
-                    in0=rstd[:, 1:2],
-                    scalar1=var[:, 1:2],
-                    scalar2=inverse_gain[:, t : t + 1],
-                    op0=ALU.mult,
-                    op1=ALU.mult,
-                )
-                nc.gpsimd.tensor_tensor(out=ratio[:, 1:2], in0=ratio[:, 0:1], in1=slope[:, 0:1], op=ALU.mult)
-                ratios[n] = ratio[:, 1:2]
-            part = small.tile([P, 2], F32, tag="part")
-            nc.gpsimd.tensor_tensor(out=part[:], in0=mean_var[:, :, 0], in1=slope[:], op=ALU.mult)
-            nc.gpsimd.tensor_tensor(out=part[:], in0=par[:, 2:4, t], in1=part[:], op=ALU.subtract)
-            shift = small.tile([P, 1], F32, tag="shift")
-            nc.gpsimd.tensor_tensor(out=shift[:], in0=part[:, 0:1], in1=part[:, 1:2], op=ALU.add)
-            slopes[n] = slope
-            shifts[n] = shift
+            slope = small.tile([P, PAIR, 2], F32, tag="slope")
+            nc.gpsimd.tensor_tensor(out=slope[:], in0=rstd[:], in1=gains[:, here, :], op=ALU.mult)
+            ratio = small.tile([P, 1], F32, tag="ratio")
+            nc.gpsimd.tensor_scalar(
+                out=ratio[:],
+                in0=rstd[:, 1, 1:2],
+                scalar1=var[:, 1, 1:2],
+                scalar2=inverse_gain[:, first + 1 : first + 2],
+                op0=ALU.mult,
+                op1=ALU.mult,
+            )
+            nc.gpsimd.tensor_tensor(out=ratio[:], in0=ratio[:], in1=slope[:, 1, 0:1], op=ALU.mult)
+            part = small.tile([P, PAIR, 2], F32, tag="part")
+            nc.gpsimd.tensor_tensor(out=part[:], in0=mean_var[:, :, :, 0], in1=slope[:], op=ALU.mult)
+            nc.gpsimd.tensor_tensor(out=part[:], in0=biases[:, here, :], in1=part[:], op=ALU.subtract)
+            shift = small.tile([P, PAIR, 1], F32, tag="shift")
+            nc.gpsimd.tensor_tensor(out=shift[:], in0=part[:, :, 0:1], in1=part[:, :, 1:2], op=ALU.add)
+            for a in range(PAIR):
+                slopes[first + a] = slope[:, a, :]
+                shifts[first + a] = shift[:, a, :]
+            ratios[first + 1] = ratio[:]
 
-        prepare_weights(0, 1)
+        prepare_weights(0)
         head_chunks = [(s, c) for s in range(2) for c in range(CHUNKS)]
         for k in range(len(head_chunks) + HEAD_LAG):
             if k < len(head_chunks):
                 prepare_chunk(*head_chunks[k])
+            if k == CHUNKS:
+                par_bank = psum.tile([P, P], BF16, tag="bank")
+                nc.tensor.transpose(par_bank[:], par_rows[:], ident_bf16[:])
+                par = const.tile([P, 4, GATES, HIDDEN_TILES], F32)
+                nc.vector.tensor_copy(
+                    out=par[:].rearrange("p q g j -> p (q g j)"), in_=par_bank[:, 0 : 4 * GATE_TILES]
+                )
+                gains = const.tile([P, GATE_TILES, 2], F32)
+                biases = const.tile([P, GATE_TILES, 2], F32)
+                for place, gate in enumerate(GATE_ORDER):
+                    for q, ordered in ((0, gains), (2, biases)):
+                        nc.gpsimd.tensor_copy(
+                            out=ordered[:].rearrange("p (j g) s -> p g j s", g=GATES)[:, place],
+                            in_=par[:, q : q + 2, gate, :].rearrange("p s j -> p j s"),
+                        )
+            if k == CHUNKS + HEAD_LAG:
+                gain_h = gains[:, :, 1]
+                more = const.tile([P, GATE_TILES], F32)
+                nc.vector.scalar_tensor_tensor(
+                    out=more[:], in0=gain_h, scalar=-1.0, in1=gain_h, op0=ALU.mult, op1=ALU.max
+                )
+                nc.vector.tensor_scalar(
+                    out=more[:], in0=more[:], scalar1=2e-18, scalar2=4e-18, op0=ALU.is_lt, op1=ALU.mult
+                )
+                nc.vector.tensor_tensor(out=gain_h, in0=gain_h, in1=more[:], op=ALU.add)
+                inverse_gain = const.tile([P, GATE_TILES], F32)
+                nc.vector.reciprocal(out=inverse_gain[:], in_=gain_h)
             if k == len(head_chunks):
-                prepare_weights(1, 1)
+                prepare_weights(1)
             if k >= HEAD_LAG:
                 s, c = head_chunks[k - HEAD_LAG]
-                (statistics_x, take_h)[s](c)
-        par_bank = psum.tile([P, P], BF16, tag="bank")
-        nc.tensor.transpose(par_bank[:], par_rows[:], ident_bf16[:])
-        par = const.tile([P, 4, GATE_TILES], F32)
-        nc.vector.tensor_copy(out=par[:].rearrange("p q t -> p (q t)"), in_=par_bank[:, 0 : 4 * GATE_TILES])
-        gain_h = par[:, 1, :]
-        more = const.tile([P, GATE_TILES], F32)
-        nc.vector.scalar_tensor_tensor(out=more[:], in0=gain_h, scalar=-1.0, in1=gain_h, op0=ALU.mult, op1=ALU.max)
-        nc.vector.tensor_scalar(out=more[:], in0=more[:], scalar1=2e-18, scalar2=4e-18, op0=ALU.is_lt, op1=ALU.mult)
-        nc.vector.tensor_tensor(out=gain_h, in0=gain_h, in1=more[:], op=ALU.add)
-        inverse_gain = const.tile([P, GATE_TILES], F32)
-        nc.vector.reciprocal(out=inverse_gain[:], in_=gain_h)
+                if s == 0:
+                    for a in range(PAIR):
+                        statistics_x(item_at[(a, c)])
+                else:
+                    take_h(item_at[(0, c)])
+                    if c > 0:
+                        kept_mean(item_at[(1, c - 1)])
+                    take_h(item_at[(1, c)])
+                    if c > 0:
+                        kept_squares(item_at[(1, c - 1)])
+        kept_mean(item_at[(1, CHUNKS - 1)])
+        kept_squares(item_at[(1, CHUNKS - 1)])
         coefficients(0)
-        prepare_weights(2, 2)
 
         next_grouped = {}
 
+        def prepare(i):
+            block, rest = divmod(i, BLOCK)
+            if not 2 <= block < BLOCKS:
+                return
+            step = rest // PAIR
+            if step == 0:
+                next_grouped[block] = new_grouped()
+            if step < PAIR:
+                transpose_weights(block, step, next_grouped[block])
+            if step == PAIR:
+                quantise_weights(block, next_grouped[block])
+
         def norm_h(i):
-            n, c = divmod(i, CHUNKS)
-            norm = sums.tile([P, CHUNK], F32, tag="norm_h")
+            n, c = tile_and_chunk(i)
+            norm = sums.tile([P, CHUNK], F32, tag="norm", bufs=NORM_TILES)
             sum_tiles[i] = norm
-            zh = project(1, n, c)
+            zh = project(1, i)
             nc.scalar.activation(
-                out=norm[:], in_=zh[:], func=ACT.Identity, scale=slopes[n][:, 1:2], bias=shifts[n][:]
+                out=norm[:], in_=zh[:], func=ACT.Identity, scale=slopes[n][:, 1:2], bias=shifts[n]
             )
 
         def add_x(i):
-            n, c = divmod(i, CHUNKS)
-            zx = project(0, n, c)
-            if not is_kept(i) and c == SPLIT_CHUNK and not is_late(i):
-                norm = sums.tile([P, CHUNK], F32, tag="norm_x", bufs=4)
-                norms_x[i] = norm
-                nc.scalar.activation(out=norm[:], in_=zx[:], func=ACT.Identity, scale=slopes[n][:, 0:1])
-            else:
-                part = sum_tiles[i][:]
-                factor = ratios[n] if is_kept(i) else slopes[n][:, 0:1]
-                nc.vector.scalar_tensor_tensor(
-                    out=part, in0=zx[:], scalar=factor, in1=part, op0=ALU.mult, op1=ALU.add
-                )
+            n, c = tile_and_chunk(i)
+            zx = project(0, i)
+            part = sum_tiles[i][:]
+            factor = ratios[n] if is_kept(i) else slopes[n][:, 0:1]
+            nc.vector.scalar_tensor_tensor(out=part, in0=zx[:], scalar=factor, in1=part, op0=ALU.mult, op1=ALU.add)
 
-        def turn(*parts):
+        def turn(part):
             bank = psum.tile([P, TILES_PER_CHUNK, P], F32, tag="bank")
             for t in range(TILES_PER_CHUNK):
-                for k, part in enumerate(parts):
-                    nc.tensor.matmul(
-                        bank[:, t, :],
-                        lhsT=part[:, t * P : (t + 1) * P],
-                        rhs=ident_f32[:],
-                        is_transpose=True,
-                        start=k == 0,
-                        stop=k == len(parts) - 1,
-                    )
+                nc.tensor.transpose(bank[:, t, :], part[:, t * P : (t + 1) * P], ident_f32[:])
             return bank
 
         def new_value(i):
@@ -386,99 +406,80 @@ def tile_cleanlstm_pa_kernel(tc, x, y, h_prev, c_prev, Wx, Wh, gx, bx, gh, bh, o
         def turned_function(i, bank):
             nc.scalar.activation(out=by_row_tile(new_value(i)[:]), in_=bank[:], func=ACT.Sigmoid)
 
-        def gate_function(i):
-            n = i // CHUNKS
+        def kept_function(i):
+            n, c = tile_and_chunk(i)
             func = ACT.Tanh if gate_of(i) == G_GATE else ACT.Sigmoid
             nc.scalar.activation(
-                out=new_value(i)[:], in_=sum_tiles[i][:], func=func, scale=slopes[n][:, 1:2], bias=shifts[n][:]
+                out=new_value(i)[:], in_=sum_tiles[i][:], func=func, scale=slopes[n][:, 1:2], bias=shifts[n]
             )
 
-        def is_late(i):
-            return i + LATE_ITEMS >= ITEMS
-
-        def pair(i, lag):
-            return [item for item in range(i - lag, i - lag + PAIR) if 0 <= item < ITEMS]
-
-        def due(i, gate, lag, short_lag, spread):
-            items = []
-            for item in range(ITEMS):
-                if gate_of(item) == gate:
-                    when = item + (short_lag if is_late(item) else lag + spread * (item % CHUNKS))
-                    if i <= when < i + PAIR:
-                        items.append(item)
-            return items
-
         def store(i, out):
-            n, c = divmod(i, CHUNKS)
+            n, c = tile_and_chunk(i)
             j = order[n][0]
             out_rows = out.rearrange("(p t) k -> p t k", t=ROW_TILES)
             nc.sync.dma_start(
                 out=out_rows[:, chunk_tiles(c), j * P : (j + 1) * P], in_=by_row_tile(values[i][:])
             )
 
-        def prepare(i):
-            n, c = divmod(i, CHUNKS)
-            if n + GATES >= GATE_TILES:
-                return
-            if c == 0:
-                next_grouped[n] = new_grouped()
-                transpose_weights(n + GATES, next_grouped[n], 0)
-            if c == 2:
-                quantise_weights(n + GATES, 1, next_grouped[n])
+        def pair(i, lag):
+            return [item for item in range(i - lag, i - lag + PAIR) if 0 <= item < ITEMS]
 
-        def engine_from(first_tile, i):
-            return nc.vector if i // CHUNKS >= first_tile else nc.gpsimd
+        def due(i, gate, lag, short_lag):
+            items = []
+            for item in range(ITEMS):
+                when = item + (short_lag if item + BLOCK >= ITEMS else lag)
+                if gate_of(item) == gate and i <= when < i + PAIR:
+                    items.append(item)
+            return items
 
-        for i in range(CHUNKS - LEAD, ITEMS + LAST_LAG, PAIR):
-            turned = []
-            for gate in (F_GATE, O_GATE):
-                for item in pair(i, LAG_TURN):
-                    if gate_of(item) == gate:
-                        parts = [sum_tiles[item]] + ([norms_x[item]] if item in norms_x else [])
-                        turned.append((item, turn(*parts)))
-            cells = [(item, turn(values[item])) for item in due(i, G_GATE, LAG_CELL, SHORT_CELL, SPREAD)]
+        for i in range(BLOCK - LEAD, ITEMS + LAST_LAG, PAIR):
+            turned = [(item, turn(sum_tiles[item])) for item in pair(i, LAG_TURN) if not is_kept(item)]
+            candidates = [(item, turn(values[item])) for item in due(i, G_GATE, LAG_CELL, SHORT_CELL)]
             for item, bank in turned:
                 turned_function(item, bank)
-            for item, bank in cells:
-                forget = item - 2 * CHUNKS
+            for item, bank in candidates:
+                forget = sibling(item, -3)
                 cell = by_row_tile(values[forget][:])
                 nc.vector.tensor_tensor(out=cell, in0=bank[:], in1=cell, op=ALU.add)
                 store(forget, out_1)
-            for item in pair(i, 0):
-                prepare(item)
+            prepare(i + LEAD + LEAD_PREPARE)
+            ahead = [item for item in pair(i, -LEAD) if item >= BLOCK]
+            taken = [item for item in pair(i, LAG_SQUARES - LEAD) if item >= BLOCK and is_kept(item)]
+            for item in taken:
+                kept_mean(item)
             for k in range(PAIR):
-                for item in pair(i, LAG_NORM_X)[k : k + 1]:
+                for item in pair(i, LAG_ADD_X)[k : k + 1]:
                     add_x(item)
-                ahead = i + k + LEAD
-                if CHUNKS <= ahead < ITEMS:
-                    statistics_x(ahead)
-                    take_h(ahead)
-                if CHUNKS <= ahead - LAG_KEPT_STATISTICS < ITEMS:
-                    kept_statistics(ahead - LAG_KEPT_STATISTICS)
-                n, c = divmod(ahead - LAG_COEFFICIENTS, CHUNKS)
-                if 1 <= n < GATE_TILES and c == CHUNKS - 1:
-                    coefficients(n)
+                for item in ahead[k : k + 1]:
+                    statistics_x(item)
+                    take_h(item)
+                if k == PAIR - 1:
+                    for item in taken:
+                        kept_squares(item)
                 for item in pair(i, 0)[k : k + 1]:
                     if not is_kept(item):
                         norm_h(item)
                 for item in pair(i, LAG_FUNCTION)[k : k + 1]:
                     if is_kept(item):
-                        gate_function(item)
-            for item in due(i, G_GATE, LAG_TANH, SHORT_CELL + 2, SPREAD):
-                nc.scalar.activation(out=values[item][:], in_=values[item - 2 * CHUNKS][:], func=ACT.Tanh)
-            for item in due(i, F_GATE, LAG_FORGET, LAG_FORGET, 0):
-                j, c = order[item // CHUNKS][0], item % CHUNKS
+                        kept_function(item)
+            for item in due(i, G_GATE, LAG_TANH, SHORT_TANH):
+                nc.scalar.activation(out=values[item][:], in_=values[sibling(item, -3)][:], func=ACT.Tanh)
+            for item in due(i, F_GATE, LAG_FORGET, LAG_FORGET):
+                n, c = tile_and_chunk(item)
+                j = order[n][0]
                 mine = by_row_tile(values[item][:])
-                cell = c_sb[:, chunk_tiles(c), j * P : (j + 1) * P]
-                engine_from(VECTOR_FORGET, item).tensor_tensor(out=mine, in0=mine, in1=cell, op=ALU.mult)
-            for item in due(i, G_GATE, LAG_CANDIDATE, LAG_CANDIDATE, 0):
-                mine = values[item][:]
-                engine_from(VECTOR_CANDIDATE, item).tensor_tensor(
-                    out=mine, in0=values[item - CHUNKS][:], in1=mine, op=ALU.mult
+                engine = nc.vector if item >= VECTOR_FORGET else nc.gpsimd
+                engine.tensor_tensor(
+                    out=mine, in0=mine, in1=c_sb[:, chunk_tiles(c), j * P : (j + 1) * P], op=ALU.mult
                 )
-            for item in due(i, O_GATE, LAG_HIDDEN, SHORT_HIDDEN, SPREAD):
+            for item in due(i, G_GATE, LAG_CANDIDATE, LAG_CANDIDATE):
                 mine = values[item][:]
-                engine_from(VECTOR_HIDDEN, item).tensor_tensor(
-                    out=mine, in0=mine, in1=values[item - CHUNKS][:], op=ALU.mult
-                )
+                nc.gpsimd.tensor_tensor(out=mine, in0=values[sibling(item, -2)][:], in1=mine, op=ALU.mult)
+            for item in due(i, O_GATE, LAG_HIDDEN, SHORT_HIDDEN):
+                mine = values[item][:]
+                engine = nc.vector if item >= VECTOR_HIDDEN else nc.gpsimd
+                engine.tensor_tensor(out=mine, in0=mine, in1=values[sibling(item, 1)][:], op=ALU.mult)
                 store(item, out_0)
+            block, rest = divmod(i + LEAD - LAG_SQUARES, BLOCK)
+            if rest == BLOCK - PAIR and 1 <= block < BLOCKS:
+                coefficients(block)

@@ -42,13 +42,13 @@ BLOCKS = ITEMS // BLOCK
 LEAD = BLOCK + 3 * PAIR
 LEAD_PREPARE = BLOCK
 LAG_SQUARES = PAIR
-HEAD_LAG = 2
+HEAD_LAG = 1
 LAG_ADD_X = 2
 LAG_TURN = 6
 LAG_FUNCTION = LAG_ADD_X + 2
 LAG_FORGET = LAG_TURN + 2
 LAG_CANDIDATE = LAG_FUNCTION
-LAG_CELL = LAG_CANDIDATE + 6
+LAG_CELL = LAG_CANDIDATE + 8
 LAG_TANH = LAG_CELL + 2
 LAG_HIDDEN = LAG_TANH + 1
 SHORT_CELL = LAG_CANDIDATE + 4
@@ -56,6 +56,7 @@ SHORT_TANH = SHORT_CELL + 2
 SHORT_HIDDEN = LAG_TURN
 VECTOR_FORGET = ITEMS - 2 * BLOCK
 VECTOR_HIDDEN = ITEMS - BLOCK
+VECTOR_CANDIDATE = ITEMS - BLOCK
 LAST_LAG = LAG_HIDDEN
 KEPT_TILES = 12
 NORM_TILES = 5
@@ -157,6 +158,9 @@ def tile_cleanlstm_pa_kernel(tc, x, y, h_prev, c_prev, Wx, Wh, gx, bx, gh, bh, o
         minus_half = const.tile([P, PAIR, 2], F32)
         nc.gpsimd.memset(minus_half[:], -0.5)
 
+        first_sigmoid = const.tile([P, 1], F32)
+        nc.scalar.activation(out=first_sigmoid[:], in_=minus_half[:, 0, 0:1], func=ACT.Sigmoid)
+
         nc.vector.tensor_copy(out=x_rows[:, :, X_WHOLE_BLOCKS : FEATURES - 1], in_=x_tail[:, :, 0:n_tail])
         nc.vector.tensor_copy(out=x_rows[:, :, FEATURES - 1 : FEATURES], in_=y_sb[:].unsqueeze(2))
 
@@ -231,11 +235,11 @@ def tile_cleanlstm_pa_kernel(tc, x, y, h_prev, c_prev, Wx, Wh, gx, bx, gh, bh, o
         stats_h = const.tile([P, BLOCKS, CHUNKS, STATS_DIM], F32)
         stats_kept = const.tile([P, BLOCKS, CHUNKS, 3], F32)
         nc.vector.memset(stats_kept[:, :, :, 0:1], float(CHUNK))
-        kept_sums = const.tile([P, ITEMS], F32)
         unread = const.tile([P, CHUNK], F32)
 
         slopes = {}
         shifts = {}
+        kept_slopes = {}
         ratios = {}
         sum_tiles = {}
         values = {}
@@ -245,22 +249,21 @@ def tile_cleanlstm_pa_kernel(tc, x, y, h_prev, c_prev, Wx, Wh, gx, bx, gh, bh, o
             z = project(0, i)
             nc.vector.bn_stats(out=stats_x[:, n, c, :], in_=z[:])
 
+        def kept_triple(i):
+            n, c = tile_and_chunk(i)
+            return stats_kept[:, n // PAIR, c, :]
+
         def take_h(i):
             n, c = tile_and_chunk(i)
             z = project(1, i)
             if is_kept(i):
                 kept = sums.tile([P, CHUNK], F32, tag="kept")
                 sum_tiles[i] = kept
-                nc.scalar.activation(out=kept[:], in_=z[:], func=ACT.Identity, accum_out=kept_sums[:, i : i + 1])
+                nc.scalar.activation(
+                    out=kept[:], in_=z[:], func=ACT.Identity, scale=1.0 / CHUNK, accum_out=kept_triple(i)[:, 1:2]
+                )
             else:
                 nc.vector.bn_stats(out=stats_h[:, n // PAIR, c, :], in_=z[:])
-
-        def kept_triple(i):
-            n, c = tile_and_chunk(i)
-            return stats_kept[:, n // PAIR, c, :]
-
-        def kept_mean(i):
-            nc.scalar.mul(out=kept_triple(i)[:, 1:2], in_=kept_sums[:, i : i + 1], mul=1.0 / CHUNK)
 
         def kept_squares(i):
             triple = kept_triple(i)
@@ -268,7 +271,7 @@ def tile_cleanlstm_pa_kernel(tc, x, y, h_prev, c_prev, Wx, Wh, gx, bx, gh, bh, o
                 out=unread[:],
                 in_=sum_tiles[i][:],
                 func=ACT.Square,
-                scale=-1.0,
+                scale=-float(CHUNK),
                 bias=triple[:, 1:2],
                 accum_out=triple[:, 2:3],
             )
@@ -288,6 +291,11 @@ def tile_cleanlstm_pa_kernel(tc, x, y, h_prev, c_prev, Wx, Wh, gx, bx, gh, bh, o
             nc.gpsimd.tensor_tensor(out=rstd[:], in0=var[:], in1=minus_half[:], op=ALU.pow)
             slope = small.tile([P, PAIR, 2], F32, tag="slope")
             nc.gpsimd.tensor_tensor(out=slope[:], in0=rstd[:], in1=gains[:, here, :], op=ALU.mult)
+            kept_slope = small.tile([P, 1], F32, tag="kept_slope")
+            nc.gpsimd.tensor_scalar(
+                out=kept_slope[:], in0=slope[:, 1, 1:2], scalar1=float(CHUNK), scalar2=0.0, op0=ALU.mult, op1=ALU.add
+            )
+            kept_slopes[first + 1] = kept_slope[:]
             ratio = small.tile([P, 1], F32, tag="ratio")
             nc.gpsimd.tensor_scalar(
                 out=ratio[:],
@@ -309,11 +317,12 @@ def tile_cleanlstm_pa_kernel(tc, x, y, h_prev, c_prev, Wx, Wh, gx, bx, gh, bh, o
             ratios[first + 1] = ratio[:]
 
         prepare_weights(0)
-        head_chunks = [(s, c) for s in range(2) for c in range(CHUNKS)]
-        for k in range(len(head_chunks) + HEAD_LAG):
-            if k < len(head_chunks):
-                prepare_chunk(*head_chunks[k])
-            if k == CHUNKS:
+        head_groups = [[(s, c), (s, c + 1)] for s in range(2) for c in range(0, CHUNKS, 2)]
+        for k in range(len(head_groups) + HEAD_LAG):
+            if k < len(head_groups):
+                for s, c in head_groups[k]:
+                    prepare_chunk(s, c)
+            if k == 2:
                 par_bank = psum.tile([P, P], BF16, tag="bank")
                 nc.tensor.transpose(par_bank[:], par_rows[:], ident_bf16[:])
                 par = const.tile([P, 4, GATES, HIDDEN_TILES], F32)
@@ -328,7 +337,7 @@ def tile_cleanlstm_pa_kernel(tc, x, y, h_prev, c_prev, Wx, Wh, gx, bx, gh, bh, o
                             out=ordered[:].rearrange("p (j g) s -> p g j s", g=GATES)[:, place],
                             in_=par[:, q : q + 2, gate, :].rearrange("p s j -> p j s"),
                         )
-            if k == CHUNKS + HEAD_LAG:
+            if k == 3:
                 gain_h = gains[:, :, 1]
                 more = const.tile([P, GATE_TILES], F32)
                 nc.vector.scalar_tensor_tensor(
@@ -340,21 +349,20 @@ def tile_cleanlstm_pa_kernel(tc, x, y, h_prev, c_prev, Wx, Wh, gx, bx, gh, bh, o
                 nc.vector.tensor_tensor(out=gain_h, in0=gain_h, in1=more[:], op=ALU.add)
                 inverse_gain = const.tile([P, GATE_TILES], F32)
                 nc.vector.reciprocal(out=inverse_gain[:], in_=gain_h)
-            if k == len(head_chunks):
+                nc.vector.tensor_scalar(
+                    out=inverse_gain[:], in0=inverse_gain[:], scalar1=1.0 / CHUNK, scalar2=0.0, op0=ALU.mult, op1=ALU.add
+                )
+            if k == len(head_groups):
                 prepare_weights(1)
-            if k >= HEAD_LAG:
-                s, c = head_chunks[k - HEAD_LAG]
+            for s, c in head_groups[k - HEAD_LAG] if k >= HEAD_LAG else ():
                 if s == 0:
                     for a in range(PAIR):
                         statistics_x(item_at[(a, c)])
                 else:
-                    take_h(item_at[(0, c)])
-                    if c > 0:
-                        kept_mean(item_at[(1, c - 1)])
-                    take_h(item_at[(1, c)])
+                    for a in range(PAIR):
+                        take_h(item_at[(a, c)])
                     if c > 0:
                         kept_squares(item_at[(1, c - 1)])
-        kept_mean(item_at[(1, CHUNKS - 1)])
         kept_squares(item_at[(1, CHUNKS - 1)])
         coefficients(0)
 
@@ -410,7 +418,7 @@ def tile_cleanlstm_pa_kernel(tc, x, y, h_prev, c_prev, Wx, Wh, gx, bx, gh, bh, o
             n, c = tile_and_chunk(i)
             func = ACT.Tanh if gate_of(i) == G_GATE else ACT.Sigmoid
             nc.scalar.activation(
-                out=new_value(i)[:], in_=sum_tiles[i][:], func=func, scale=slopes[n][:, 1:2], bias=shifts[n]
+                out=new_value(i)[:], in_=sum_tiles[i][:], func=func, scale=kept_slopes[n], bias=shifts[n]
             )
 
         def store(i, out):
@@ -445,8 +453,6 @@ def tile_cleanlstm_pa_kernel(tc, x, y, h_prev, c_prev, Wx, Wh, gx, bx, gh, bh, o
             prepare(i + LEAD + LEAD_PREPARE)
             ahead = [item for item in pair(i, -LEAD) if item >= BLOCK]
             taken = [item for item in pair(i, LAG_SQUARES - LEAD) if item >= BLOCK and is_kept(item)]
-            for item in taken:
-                kept_mean(item)
             for k in range(PAIR):
                 for item in pair(i, LAG_ADD_X)[k : k + 1]:
                     add_x(item)
@@ -474,7 +480,8 @@ def tile_cleanlstm_pa_kernel(tc, x, y, h_prev, c_prev, Wx, Wh, gx, bx, gh, bh, o
                 )
             for item in due(i, G_GATE, LAG_CANDIDATE, LAG_CANDIDATE):
                 mine = values[item][:]
-                nc.gpsimd.tensor_tensor(out=mine, in0=values[sibling(item, -2)][:], in1=mine, op=ALU.mult)
+                engine = nc.vector if item >= VECTOR_CANDIDATE and item % PAIR == 1 else nc.gpsimd
+                engine.tensor_tensor(out=mine, in0=values[sibling(item, -2)][:], in1=mine, op=ALU.mult)
             for item in due(i, O_GATE, LAG_HIDDEN, SHORT_HIDDEN):
                 mine = values[item][:]
                 engine = nc.vector if item >= VECTOR_HIDDEN else nc.gpsimd

@@ -44,7 +44,7 @@ LEAD_PREPARE = BLOCK
 LAG_SQUARES = PAIR
 HEAD_LAG = 1
 LAG_ADD_X = 2
-LAG_TURN = 6
+LAG_TURN = 4
 LAG_FUNCTION = LAG_ADD_X + 2
 LAG_FORGET = LAG_TURN + 2
 LAG_CANDIDATE = LAG_FUNCTION
@@ -53,7 +53,7 @@ LAG_TANH = LAG_CELL + 2
 LAG_HIDDEN = LAG_TANH + 1
 SHORT_CELL = LAG_CANDIDATE + 4
 SHORT_TANH = SHORT_CELL + 2
-SHORT_HIDDEN = LAG_TURN
+SHORT_HIDDEN = SHORT_TANH - CHUNKS
 VECTOR_FORGET = ITEMS - 2 * BLOCK
 VECTOR_HIDDEN = ITEMS - BLOCK
 VECTOR_CANDIDATE = ITEMS - BLOCK
@@ -441,16 +441,6 @@ def tile_cleanlstm_pa_kernel(tc, x, y, h_prev, c_prev, Wx, Wh, gx, bx, gh, bh, o
             return items
 
         for i in range(BLOCK - LEAD, ITEMS + LAST_LAG, PAIR):
-            turned = [(item, turn(sum_tiles[item])) for item in pair(i, LAG_TURN) if not is_kept(item)]
-            candidates = [(item, turn(values[item])) for item in due(i, G_GATE, LAG_CELL, SHORT_CELL)]
-            for item, bank in turned:
-                turned_function(item, bank)
-            for item, bank in candidates:
-                forget = sibling(item, -3)
-                cell = by_row_tile(values[forget][:])
-                nc.vector.tensor_tensor(out=cell, in0=bank[:], in1=cell, op=ALU.add)
-                store(forget, out_1)
-            prepare(i + LEAD + LEAD_PREPARE)
             ahead = [item for item in pair(i, -LEAD) if item >= BLOCK]
             taken = [item for item in pair(i, LAG_SQUARES - LEAD) if item >= BLOCK and is_kept(item)]
             for k in range(PAIR):
@@ -468,6 +458,16 @@ def tile_cleanlstm_pa_kernel(tc, x, y, h_prev, c_prev, Wx, Wh, gx, bx, gh, bh, o
                 for item in pair(i, LAG_FUNCTION)[k : k + 1]:
                     if is_kept(item):
                         kept_function(item)
+            turned = [(item, turn(sum_tiles[item])) for item in pair(i, LAG_TURN) if not is_kept(item)]
+            candidates = [(item, turn(values[item])) for item in due(i, G_GATE, LAG_CELL, SHORT_CELL)]
+            for item, bank in turned:
+                turned_function(item, bank)
+            for item, bank in candidates:
+                forget = sibling(item, -3)
+                cell = by_row_tile(values[forget][:])
+                nc.vector.tensor_tensor(out=cell, in0=bank[:], in1=cell, op=ALU.add)
+                store(forget, out_1)
+            prepare(i + LEAD + LEAD_PREPARE)
             for item in due(i, G_GATE, LAG_TANH, SHORT_TANH):
                 nc.scalar.activation(out=values[item][:], in_=values[sibling(item, -3)][:], func=ACT.Tanh)
             for item in due(i, F_GATE, LAG_FORGET, LAG_FORGET):
@@ -480,7 +480,7 @@ def tile_cleanlstm_pa_kernel(tc, x, y, h_prev, c_prev, Wx, Wh, gx, bx, gh, bh, o
                 )
             for item in due(i, G_GATE, LAG_CANDIDATE, LAG_CANDIDATE):
                 mine = values[item][:]
-                engine = nc.vector if item >= VECTOR_CANDIDATE and item % PAIR == 1 else nc.gpsimd
+                engine = nc.vector if item >= VECTOR_CANDIDATE and item % PAIR == 0 else nc.gpsimd
                 engine.tensor_tensor(out=mine, in0=values[sibling(item, -2)][:], in1=mine, op=ALU.mult)
             for item in due(i, O_GATE, LAG_HIDDEN, SHORT_HIDDEN):
                 mine = values[item][:]

@@ -40,7 +40,6 @@ BLOCK = PAIR * CHUNKS
 BLOCKS = ITEMS // BLOCK
 
 LEAD = BLOCK + 3 * PAIR
-LEAD_PREPARE = BLOCK
 LAG_SQUARES = PAIR
 HEAD_LAG = 1
 LAG_ADD_X = 2
@@ -369,15 +368,15 @@ def tile_cleanlstm_pa_kernel(tc, x, y, h_prev, c_prev, Wx, Wh, gx, bx, gh, bh, o
         next_grouped = {}
 
         def prepare(i):
-            block, rest = divmod(i, BLOCK)
-            if not 2 <= block < BLOCKS:
+            turns = (i + LEAD - BLOCK) // PAIR
+            block, step = turns // 2 + 2, turns % 2
+            if block >= BLOCKS:
                 return
-            step = rest // PAIR
             if step == 0:
                 next_grouped[block] = new_grouped()
-            if step < PAIR:
-                transpose_weights(block, step, next_grouped[block])
-            if step == PAIR:
+                for a in range(PAIR):
+                    transpose_weights(block, a, next_grouped[block])
+            else:
                 quantise_weights(block, next_grouped[block])
 
         def norm_h(i):
@@ -467,7 +466,7 @@ def tile_cleanlstm_pa_kernel(tc, x, y, h_prev, c_prev, Wx, Wh, gx, bx, gh, bh, o
                 cell = by_row_tile(values[forget][:])
                 nc.vector.tensor_tensor(out=cell, in0=bank[:], in1=cell, op=ALU.add)
                 store(forget, out_1)
-            prepare(i + LEAD + LEAD_PREPARE)
+            prepare(i)
             for item in due(i, G_GATE, LAG_TANH, SHORT_TANH):
                 nc.scalar.activation(out=values[item][:], in_=values[sibling(item, -3)][:], func=ACT.Tanh)
             for item in due(i, F_GATE, LAG_FORGET, LAG_FORGET):

from contextlib import ExitStack

import concourse.mybir as mybir
from concourse.masks import make_identity

F32 = mybir.dt.float32
BF16 = mybir.dt.bfloat16
U32 = mybir.dt.uint32
U8 = mybir.dt.uint8
FP8X4 = mybir.dt.float8_e4m3fn_x4
ACT = mybir.ActivationFunctionType
ALU = mybir.AluOpType

P = 128
PACK = 4
BATCH = 2048
FEATURES = P * PACK
HIDDEN = 512
GATES = 4
F_GATE, I_GATE, O_GATE, G_GATE = 0, 1, 2, 3
EPS = 1e-5

ROW_TILES = BATCH // P
CHUNK = 512
CHUNKS = BATCH // CHUNK
TILES_PER_CHUNK = CHUNK // P
HIDDEN_TILES = HIDDEN // P
GATE_TILES = GATES * HIDDEN_TILES
WORDS = FEATURES // 2
X_WHOLE_BLOCKS = 496
STATS_DIM = 6

FLOPS = 2 * 2 * BATCH * GATES * HIDDEN * FEATURES

GATE_ORDER = (F_GATE, I_GATE, O_GATE, G_GATE)
KEPT_GATES = (I_GATE, G_GATE)
PAIR = 2
ITEMS = GATE_TILES * CHUNKS
BLOCK = PAIR * CHUNKS
BLOCKS = ITEMS // BLOCK

LEAD = BLOCK + 3 * PAIR
LAG_SQUARES = PAIR
HEAD_LAG = 1
LAG_ADD_X = 2
LAG_TURN = 4
LAG_FUNCTION = LAG_ADD_X + 2
LAG_FORGET = LAG_TURN + 2
LAG_CANDIDATE = LAG_FUNCTION
LAG_CELL = LAG_CANDIDATE + 8
LAG_TANH = LAG_CELL + 2
LAG_HIDDEN = LAG_TANH + 1
SHORT_CELL = LAG_CANDIDATE + 4
SHORT_TANH = SHORT_CELL + 2
SHORT_HIDDEN = SHORT_TANH - CHUNKS
VECTOR_FORGET = ITEMS - 2 * BLOCK
VECTOR_HIDDEN = ITEMS - BLOCK
VECTOR_CANDIDATE = ITEMS - BLOCK
LAST_LAG = LAG_HIDDEN
KEPT_TILES = 12
NORM_TILES = 5
VALUE_TILES = {F_GATE: 9, I_GATE: 6, O_GATE: 7, G_GATE: 7}


def tile_cleanlstm_pa_kernel(tc, x, y, h_prev, c_prev, Wx, Wh, gx, bx, gh, bh, out_0, out_1):
    nc = tc.nc
    with ExitStack() as ctx:
        ctx.enter_context(tc.manual_schedule())
        const = ctx.enter_context(tc.tile_pool(name="const", bufs=1))
        raw = ctx.enter_context(tc.tile_pool(name="raw", bufs=1))
        keep = ctx.enter_context(tc.tile_pool(name="keep", bufs=1))
        stage = ctx.enter_context(tc.tile_pool(name="stage", bufs=3))
        small = ctx.enter_context(tc.tile_pool(name="small", bufs=4))
        sums = ctx.enter_context(tc.tile_pool(name="sums", bufs=KEPT_TILES))
        gates = ctx.enter_context(tc.tile_pool(name="gates", bufs=8))
        psum = ctx.enter_context(tc.psum_pool(name="psum", bufs=8))

        def chunk_cols(c):
            return slice(c * CHUNK, (c + 1) * CHUNK)

        def chunk_tiles(c):
            return slice(c * TILES_PER_CHUNK, (c + 1) * TILES_PER_CHUNK)

        order = [(j, gate) for j in range(HIDDEN_TILES) for gate in GATE_ORDER]

        def tile_and_chunk(i):
            block, rest = divmod(i, BLOCK)
            if block == BLOCKS - 1:
                return block * PAIR + 1 - rest // CHUNKS, rest % CHUNKS
            return block * PAIR + rest % PAIR, rest // PAIR

        item_at = {}
        for i in range(ITEMS):
            item_at[tile_and_chunk(i)] = i

        def sibling(i, tiles):
            n, c = tile_and_chunk(i)
            return item_at[(n + tiles, c)]

        def gate_of(i):
            return order[tile_and_chunk(i)[0]][1]

        def is_kept(i):
            return gate_of(i) in KEPT_GATES

        x_sb = raw.tile([P, ROW_TILES * FEATURES], BF16)
        x_rows = x_sb[:].rearrange("p (t k) -> p t k", t=ROW_TILES)
        x_dram = x.rearrange("(p t) k -> p t k", t=ROW_TILES)
        x_tail = raw.tile([P, ROW_TILES, 16], BF16)
        y_sb = raw.tile([P, ROW_TILES], BF16)
        h_sb = raw.tile([P, ROW_TILES * FEATURES], BF16)
        h_rows = h_sb[:].rearrange("p (t k) -> p t k", t=ROW_TILES)
        h_dram = h_prev.rearrange("(p t) k -> p t k", t=ROW_TILES)
        c_sb = raw.tile([P, ROW_TILES, HIDDEN], BF16)
        wx_sb = raw.tile([P, HIDDEN_TILES * GATES * FEATURES], BF16)
        wh_sb = raw.tile([P, HIDDEN_TILES * GATES * FEATURES], BF16)
        wx_rows = wx_sb[:].rearrange("p (j g k) -> p j g k", j=HIDDEN_TILES, g=GATES)
        wh_rows = wh_sb[:].rearrange("p (j g k) -> p j g k", j=HIDDEN_TILES, g=GATES)
        wx_dram = Wx.rearrange("(g j p) k -> p j g k", g=GATES, j=HIDDEN_TILES)
        wh_dram = Wh.rearrange("(g j p) k -> p j g k", g=GATES, j=HIDDEN_TILES)

        n_tail = FEATURES - 1 - X_WHOLE_BLOCKS
        nc.scalar.dma_start(out=x_tail[:, :, 0:n_tail], in_=x_dram[:, :, X_WHOLE_BLOCKS : FEATURES - 1])
        nc.scalar.dma_start(out=y_sb[:], in_=y.rearrange("(p t) o -> p (t o)", t=ROW_TILES))
        par_rows = const.tile([P, P], BF16)
        nc.vector.memset(par_rows[:], 0.0)
        for q, vec in enumerate((gx, gh, bx, bh)):
            nc.scalar.dma_start(
                out=par_rows[q * GATE_TILES : (q + 1) * GATE_TILES, :], in_=vec.rearrange("(t p) -> t p", p=P)
            )

        def load_weights(j, gate):
            nc.sync.dma_start(out=wx_rows[:, j, gate], in_=wx_dram[:, j, gate])
            nc.sync.dma_start(out=wh_rows[:, j, gate], in_=wh_dram[:, j, gate])

        for gate in GATE_ORDER[0:PAIR]:
            load_weights(0, gate)
        for c in range(CHUNKS):
            nc.sync.dma_start(
                out=x_rows[:, chunk_tiles(c), 0:X_WHOLE_BLOCKS], in_=x_dram[:, chunk_tiles(c), 0:X_WHOLE_BLOCKS]
            )
        for c in range(CHUNKS):
            nc.sync.dma_start(out=h_rows[:, chunk_tiles(c), :], in_=h_dram[:, chunk_tiles(c), :])
        for gate in GATE_ORDER[PAIR:]:
            load_weights(0, gate)
        nc.sync.dma_start(out=wx_rows[:, 1], in_=wx_dram[:, 1])
        nc.sync.dma_start(out=wh_rows[:, 1], in_=wh_dram[:, 1])
        nc.sync.dma_start(out=c_sb[:], in_=c_prev.rearrange("(p t) k -> p t k", t=ROW_TILES))
        for j in range(2, HIDDEN_TILES):
            nc.sync.dma_start(out=wx_rows[:, j], in_=wx_dram[:, j])
            nc.sync.dma_start(out=wh_rows[:, j], in_=wh_dram[:, j])

        ident_f32 = const.tile([P, P], F32)
        make_identity(nc, ident_f32[:])
        ident_bf16 = const.tile([P, P], BF16)
        make_identity(nc, ident_bf16[:])
        minus_half = const.tile([P, PAIR, 2], F32)
        nc.gpsimd.memset(minus_half[:], -0.5)

        first_sigmoid = const.tile([P, 1], F32)
        nc.scalar.activation(out=first_sigmoid[:], in_=minus_half[:, 0, 0:1], func=ACT.Sigmoid)

        nc.vector.tensor_copy(out=x_rows[:, :, X_WHOLE_BLOCKS : FEATURES - 1], in_=x_tail[:, :, 0:n_tail])
        nc.vector.tensor_copy(out=x_rows[:, :, FEATURES - 1 : FEATURES], in_=y_sb[:].unsqueeze(2))

        x_codes = keep.tile([P, BATCH], U32, align_bytes=64)
        x_scales = keep.tile([P, BATCH], U8, align_bytes=64)
        h_codes = keep.tile([P, BATCH], U32, align_bytes=64)
        h_scales = keep.tile([P, BATCH], U8, align_bytes=64)
        w_codes = keep.tile([P, GATE_TILES * 2 * P], U32, align_bytes=64)
        w_scales = keep.tile([P, GATE_TILES * 2 * P], U8, align_bytes=64)

        x_words = x_sb[:].bitcast(F32).rearrange("p (t w) -> p t w", w=WORDS)
        h_words = h_sb[:].bitcast(F32).rearrange("p (t w) -> p t w", w=WORDS)
        wx_words = wx_sb[:].bitcast(F32).rearrange("p (t w) -> p t w", w=WORDS)
        wh_words = wh_sb[:].bitcast(F32).rearrange("p (t w) -> p t w", w=WORDS)
        activations = ((x_words, x_codes, x_scales), (h_words, h_codes, h_scales))

        def new_grouped():
            grouped = stage.tile([P, CHUNK * PACK], BF16, tag="grouped", align_bytes=64)
            return grouped

        def transpose_256_rows(row_blocks, grouped, a):
            grouped_words = grouped[:].bitcast(F32).rearrange("p (a t r u) -> p a t r u", a=2, t=2, u=2)
            bank = psum.tile([P, 2, 2, P], F32, tag="bank")
            for t, words in enumerate(row_blocks):
                for u in range(2):
                    nc.tensor.transpose(bank[:, t, u, :], words[:, u : 2 * P : 2], ident_f32[:])
            nc.scalar.copy(out=grouped_words[:, a], in_=bank[:].rearrange("p t u r -> p t r u"))

        def quantise(grouped, codes, scales, cols):
            nc.vector.quantize_mx(out=codes[:, cols].bitcast(FP8X4), scales=scales[:, cols], in_=grouped[:])

        def prepare_chunk(s, c):
            words, codes, scales = activations[s]
            grouped = new_grouped()
            for a in range(2):
                first = c * TILES_PER_CHUNK + 2 * a
                transpose_256_rows((words[:, first], words[:, first + 1]), grouped, a)
            quantise(grouped, codes, scales, chunk_cols(c))

        def transpose_weights(block, a, grouped):
            j, gate = order[block * PAIR + a]
            row_tile = j * GATES + gate
            transpose_256_rows((wx_words[:, row_tile], wh_words[:, row_tile]), grouped, a)

        def quantise_weights(block, grouped):
            width = PAIR * 2 * P
            quantise(grouped, w_codes, w_scales, slice(block * width, (block + 1) * width))

        def prepare_weights(block):
            grouped = new_grouped()
            for a in range(PAIR):
                transpose_weights(block, a, grouped)
            quantise_weights(block, grouped)

        def project(s, i):
            n, c = tile_and_chunk(i)
            w_cols = slice((n * 2 + s) * P, (n * 2 + s + 1) * P)
            words, codes, scales = activations[s]
            z = psum.tile([P, CHUNK], F32, tag="bank")
            nc.tensor.matmul_mx(
                out=z[:],
                lhsT=w_codes[:, w_cols].bitcast(FP8X4),
                lhsT_scale=w_scales[:, w_cols],
                rhs=codes[:, chunk_cols(c)].bitcast(FP8X4),
                rhs_scale=scales[:, chunk_cols(c)],
                start=True,
                stop=True,
            )
            return z

        stats_x = const.tile([P, GATE_TILES, CHUNKS, STATS_DIM], F32)
        stats_h = const.tile([P, BLOCKS, CHUNKS, STATS_DIM], F32)
        stats_kept = const.tile([P, BLOCKS, CHUNKS, 3], F32)
        nc.vector.memset(stats_kept[:, :, :, 0:1], float(CHUNK))
        unread = const.tile([P, CHUNK], F32)

        slopes = {}
        shifts = {}
        kept_slopes = {}
        ratios = {}
        sum_tiles = {}
        values = {}

        def statistics_x(i):
            n, c = tile_and_chunk(i)
            z = project(0, i)
            nc.vector.bn_stats(out=stats_x[:, n, c, :], in_=z[:])

        def kept_triple(i):
            n, c = tile_and_chunk(i)
            return stats_kept[:, n // PAIR, c, :]

        def take_h(i):
            n, c = tile_and_chunk(i)
            z = project(1, i)
            if is_kept(i):
                kept = sums.tile([P, CHUNK], F32, tag="kept")
                sum_tiles[i] = kept
                nc.scalar.activation(
                    out=kept[:], in_=z[:], func=ACT.Identity, scale=1.0 / CHUNK, accum_out=kept_triple(i)[:, 1:2]
                )
            else:
                nc.vector.bn_stats(out=stats_h[:, n // PAIR, c, :], in_=z[:])

        def kept_squares(i):
            triple = kept_triple(i)
            nc.scalar.activation(
                out=unread[:],
                in_=sum_tiles[i][:],
                func=ACT.Square,
                scale=-float(CHUNK),
                bias=triple[:, 1:2],
                accum_out=triple[:, 2:3],
            )

        def coefficients(block):
            first = block * PAIR
            here = slice(first, first + PAIR)
            mean_var = small.tile([P, PAIR, 2, 2], F32, tag="mean_var")
            for a, of_h in enumerate((stats_h, stats_kept)):
                for s, triples in enumerate((stats_x[:, first + a], of_h[:, block])):
                    nc.vector.bn_aggr(out=mean_var[:, a, s, :], in_=triples.rearrange("p c v -> p (c v)"))
            var = small.tile([P, PAIR, 2], F32, tag="var")
            nc.gpsimd.tensor_scalar(
                out=var[:], in0=mean_var[:, :, :, 1], scalar1=1.0, scalar2=EPS, op0=ALU.mult, op1=ALU.add
            )
            rstd = small.tile([P, PAIR, 2], F32, tag="rstd")
            nc.gpsimd.tensor_tensor(out=rstd[:], in0=var[:], in1=minus_half[:], op=ALU.pow)
            slope = small.tile([P, PAIR, 2], F32, tag="slope")
            nc.gpsimd.tensor_tensor(out=slope[:], in0=rstd[:], in1=gains[:, here, :], op=ALU.mult)
            kept_slope = small.tile([P, 1], F32, tag="kept_slope")
            nc.gpsimd.tensor_scalar(
                out=kept_slope[:], in0=slope[:, 1, 1:2], scalar1=float(CHUNK), scalar2=0.0, op0=ALU.mult, op1=ALU.add
            )
            kept_slopes[first + 1] = kept_slope[:]
            ratio = small.tile([P, 1], F32, tag="ratio")
            nc.gpsimd.tensor_scalar(
                out=ratio[:],
                in0=rstd[:, 1, 1:2],
                scalar1=var[:, 1, 1:2],
                scalar2=inverse_gain[:, first + 1 : first + 2],
                op0=ALU.mult,
                op1=ALU.mult,
            )
            nc.gpsimd.tensor_tensor(out=ratio[:], in0=ratio[:], in1=slope[:, 1, 0:1], op=ALU.mult)
            part = small.tile([P, PAIR, 2], F32, tag="part")
            nc.gpsimd.tensor_tensor(out=part[:], in0=mean_var[:, :, :, 0], in1=slope[:], op=ALU.mult)
            nc.gpsimd.tensor_tensor(out=part[:], in0=biases[:, here, :], in1=part[:], op=ALU.subtract)
            shift = small.tile([P, PAIR, 1], F32, tag="shift")
            nc.gpsimd.tensor_tensor(out=shift[:], in0=part[:, :, 0:1], in1=part[:, :, 1:2], op=ALU.add)
            for a in range(PAIR):
                slopes[first + a] = slope[:, a, :]
                shifts[first + a] = shift[:, a, :]
            ratios[first + 1] = ratio[:]

        prepare_weights(0)
        head_groups = [[(s, c), (s, c + 1)] for s in range(2) for c in range(0, CHUNKS, 2)]
        for k in range(len(head_groups) + HEAD_LAG):
            if k < len(head_groups):
                for s, c in head_groups[k]:
                    prepare_chunk(s, c)
            if k == 2:
                par_bank = psum.tile([P, P], BF16, tag="bank")
                nc.tensor.transpose(par_bank[:], par_rows[:], ident_bf16[:])
                par = const.tile([P, 4, GATES, HIDDEN_TILES], F32)
                nc.vector.tensor_copy(
                    out=par[:].rearrange("p q g j -> p (q g j)"), in_=par_bank[:, 0 : 4 * GATE_TILES]
                )
                gains = const.tile([P, GATE_TILES, 2], F32)
                biases = const.tile([P, GATE_TILES, 2], F32)
                for place, gate in enumerate(GATE_ORDER):
                    for q, ordered in ((0, gains), (2, biases)):
                        nc.gpsimd.tensor_copy(
                            out=ordered[:].rearrange("p (j g) s -> p g j s", g=GATES)[:, place],
                            in_=par[:, q : q + 2, gate, :].rearrange("p s j -> p j s"),
                        )
            if k == 3:
                gain_h = gains[:, :, 1]
                more = const.tile([P, GATE_TILES], F32)
                nc.vector.scalar_tensor_tensor(
                    out=more[:], in0=gain_h, scalar=-1.0, in1=gain_h, op0=ALU.mult, op1=ALU.max
                )
                nc.vector.tensor_scalar(
                    out=more[:], in0=more[:], scalar1=2e-18, scalar2=4e-18, op0=ALU.is_lt, op1=ALU.mult
                )
                nc.vector.tensor_tensor(out=gain_h, in0=gain_h, in1=more[:], op=ALU.add)
                inverse_gain = const.tile([P, GATE_TILES], F32)
                nc.vector.reciprocal(out=inverse_gain[:], in_=gain_h)
                nc.vector.tensor_scalar(
                    out=inverse_gain[:], in0=inverse_gain[:], scalar1=1.0 / CHUNK, scalar2=0.0, op0=ALU.mult, op1=ALU.add
                )
            if k == len(head_groups):
                prepare_weights(1)
            for s, c in head_groups[k - HEAD_LAG] if k >= HEAD_LAG else ():
                if s == 0:
                    for a in range(PAIR):
                        statistics_x(item_at[(a, c)])
                else:
                    for a in range(PAIR):
                        take_h(item_at[(a, c)])
                    if c > 0:
                        kept_squares(item_at[(1, c - 1)])
        kept_squares(item_at[(1, CHUNKS - 1)])
        coefficients(0)

        next_grouped = {}

        def prepare(i):
            turns = (i + LEAD - BLOCK) // PAIR
            block, step = turns // 2 + 2, turns % 2
            if block >= BLOCKS:
                return
            if step == 0:
                next_grouped[block] = new_grouped()
                for a in range(PAIR):
                    transpose_weights(block, a, next_grouped[block])
            else:
                quantise_weights(block, next_grouped[block])

        def norm_h(i):
            n, c = tile_and_chunk(i)
            norm = sums.tile([P, CHUNK], F32, tag="norm", bufs=NORM_TILES)
            sum_tiles[i] = norm
            zh = project(1, i)
            nc.scalar.activation(
                out=norm[:], in_=zh[:], func=ACT.Identity, scale=slopes[n][:, 1:2], bias=shifts[n]
            )

        def add_x(i):
            n, c = tile_and_chunk(i)
            zx = project(0, i)
            part = sum_tiles[i][:]
            factor = ratios[n] if is_kept(i) else slopes[n][:, 0:1]
            nc.vector.scalar_tensor_tensor(out=part, in0=zx[:], scalar=factor, in1=part, op0=ALU.mult, op1=ALU.add)

        def turn(part):
            bank = psum.tile([P, TILES_PER_CHUNK, P], F32, tag="bank")
            for t in range(TILES_PER_CHUNK):
                nc.tensor.transpose(bank[:, t, :], part[:, t * P : (t + 1) * P], ident_f32[:])
            return bank

        def new_value(i):
            gate = gate_of(i)
            value = gates.tile([P, CHUNK], F32, tag="gate%d" % gate, bufs=VALUE_TILES[gate])
            values[i] = value
            return value

        def by_row_tile(ap):
            return ap.rearrange("p (t f) -> p t f", t=TILES_PER_CHUNK)

        def turned_function(i, bank):
            nc.scalar.activation(out=by_row_tile(new_value(i)[:]), in_=bank[:], func=ACT.Sigmoid)

        def kept_function(i):
            n, c = tile_and_chunk(i)
            func = ACT.Tanh if gate_of(i) == G_GATE else ACT.Sigmoid
            nc.scalar.activation(
                out=new_value(i)[:], in_=sum_tiles[i][:], func=func, scale=kept_slopes[n], bias=shifts[n]
            )

        def store(i, out):
            n, c = tile_and_chunk(i)
            j = order[n][0]
            out_rows = out.rearrange("(p t) k -> p t k", t=ROW_TILES)
            nc.sync.dma_start(
                out=out_rows[:, chunk_tiles(c), j * P : (j + 1) * P], in_=by_row_tile(values[i][:])
            )

        def pair(i, lag):
            return [item for item in range(i - lag, i - lag + PAIR) if 0 <= item < ITEMS]

        def due(i, gate, lag, short_lag):
            items = []
            for item in range(ITEMS):
                when = item + (short_lag if item + BLOCK >= ITEMS else lag)
                if gate_of(item) == gate and i <= when < i + PAIR:
                    items.append(item)
            return items

        for i in range(BLOCK - LEAD, ITEMS + LAST_LAG, PAIR):
            ahead = [item for item in pair(i, -LEAD) if item >= BLOCK]
            taken = [item for item in pair(i, LAG_SQUARES - LEAD) if item >= BLOCK and is_kept(item)]
            for k in range(PAIR):
                for item in pair(i, LAG_ADD_X)[k : k + 1]:
                    add_x(item)
                for item in ahead[k : k + 1]:
                    statistics_x(item)
                    take_h(item)
                if k == PAIR - 1:
                    for item in taken:
                        kept_squares(item)
                for item in pair(i, 0)[k : k + 1]:
                    if not is_kept(item):
                        norm_h(item)
                for item in pair(i, LAG_FUNCTION)[k : k + 1]:
                    if is_kept(item):
                        kept_function(item)
            turned = [(item, turn(sum_tiles[item])) for item in pair(i, LAG_TURN) if not is_kept(item)]
            candidates = [(item, turn(values[item])) for item in due(i, G_GATE, LAG_CELL, SHORT_CELL)]
            for item, bank in turned:
                turned_function(item, bank)
            for item, bank in candidates:
                forget = sibling(item, -3)
                cell = by_row_tile(values[forget][:])
                nc.vector.tensor_tensor(out=cell, in0=bank[:], in1=cell, op=ALU.add)
                store(forget, out_1)
            prepare(i)
            for item in due(i, G_GATE, LAG_TANH, SHORT_TANH):
                nc.scalar.activation(out=values[item][:], in_=values[sibling(item, -3)][:], func=ACT.Tanh)
            for item in due(i, F_GATE, LAG_FORGET, LAG_FORGET):
                n, c = tile_and_chunk(item)
                j = order[n][0]
                mine = by_row_tile(values[item][:])
                engine = nc.vector if item >= VECTOR_FORGET else nc.gpsimd
                engine.tensor_tensor(
                    out=mine, in0=mine, in1=c_sb[:, chunk_tiles(c), j * P : (j + 1) * P], op=ALU.mult
                )
            for item in due(i, G_GATE, LAG_CANDIDATE, LAG_CANDIDATE):
                mine = values[item][:]
                engine = nc.vector if item >= VECTOR_CANDIDATE and item % PAIR == 0 else nc.gpsimd
                engine.tensor_tensor(out=mine, in0=values[sibling(item, -2)][:], in1=mine, op=ALU.mult)
            for item in due(i, O_GATE, LAG_HIDDEN, SHORT_HIDDEN):
                mine = values[item][:]
                engine = nc.vector if item >= VECTOR_HIDDEN else nc.gpsimd
                engine.tensor_tensor(out=mine, in0=mine, in1=values[sibling(item, 1)][:], op=ALU.mult)
                store(item, out_0)
            block, rest = divmod(i + LEAD - LAG_SQUARES, BLOCK)
            if rest == BLOCK - PAIR and 1 <= block < BLOCKS:
                coefficients(block)
